import numpy as np
import ml_dtypes


def mxq(x, axis, fmt="e4m3"):
    dtype, down = {"e4m3": (ml_dtypes.float8_e4m3fn, 7), "e5m2": (ml_dtypes.float8_e5m2, 14)}[fmt]
    v = np.moveaxis(np.asarray(x, np.float32).astype(ml_dtypes.bfloat16).astype(np.float64), axis, -1)
    blocks = v.reshape(v.shape[:-1] + (-1, 32))
    amax = np.abs(blocks).max(-1, keepdims=True)
    byte = np.maximum(np.where(amax > 0, np.frexp(amax)[1] - 1 + 127, 0) - down, 1)
    scale = np.exp2(byte - 127.0)
    codes = (blocks / scale).astype(np.float32).astype(dtype).astype(np.float64)
    return np.moveaxis((codes * scale).reshape(v.shape), -1, axis)


WIDE = False


def mx_kscale(k):
    if not WIDE:
        return np.ones(k)
    levels = np.array([10, -10, 5, -5, 0])
    if k % 512:
        return np.exp2(np.random.permutation(np.resize(levels, k // 32))).repeat(32)
    a = np.empty((k // 512, 16))
    for p in range(k // 512):
        a[p, :8] = np.random.permutation(np.resize(levels, 8))
        for g in range(8):
            far = levels[np.abs(levels - a[p, g]) >= 10]
            a[p, g + 8] = far[np.random.randint(len(far))]
    return np.exp2(a.ravel()).repeat(32)


BF16 = ml_dtypes.bfloat16


def bf(x):
    return np.asarray(x, np.float32).astype(BF16)


def f64(x):
    return np.asarray(x).astype(np.float64)


B, S, H, I, R = 4, 64, 2048, 7168, 512
EPS = 1e-05


def rmsnorm(h, w):
    var = np.mean(h * h, axis=-1, keepdims=True)
    return h * (1.0 / np.sqrt(var + EPS)) * w


def silu(v):
    return v / (1.0 + np.exp(-v))


def setup_inputs():
    s, t = mx_kscale(H), mx_kscale(R)
    return {"x": bf(np.random.standard_normal((B, S, H))),
            "residual": bf(np.random.standard_normal((B, S, H))),
            "ln_w": bf((1.0 + 0.1 * np.random.standard_normal(H)) * s),
            "w_gate_v": bf(np.random.standard_normal((H, R)) / np.sqrt(H) / s[:, None] * t),
            "w_gate_u": bf(np.random.standard_normal((R, I)) / np.sqrt(R) / t[:, None]),
            "w_up_v": bf(np.random.standard_normal((H, R)) / np.sqrt(H) / s[:, None] * t),
            "w_up_u": bf(np.random.standard_normal((R, I)) / np.sqrt(R) / t[:, None])}


def reference(x, residual, ln_w, w_gate_v, w_gate_u, w_up_v, w_up_u):
    h = f64(x) + f64(residual)
    n = rmsnorm(h, f64(ln_w))
    nq = mxq(n, 2, "e4m3")
    gate_r = nq @ mxq(f64(w_gate_v), 0, "e4m3")
    up_r = nq @ mxq(f64(w_up_v), 0, "e4m3")
    gate = silu(mxq(gate_r, 2, "e4m3") @ mxq(f64(w_gate_u), 0, "e4m3"))
    up = mxq(up_r, 2, "e4m3") @ mxq(f64(w_up_u), 0, "e4m3")
    return gate * up

@@ -1,0 +1,374 @@
+from contextlib import ExitStack
+
+import concourse.mybir as mybir
+from concourse.masks import make_identity
+
+F32 = mybir.dt.float32
+BF16 = mybir.dt.bfloat16
+U32 = mybir.dt.uint32
+U8 = mybir.dt.uint8
+FP8X4 = mybir.dt.float8_e4m3fn_x4
+ACT = mybir.ActivationFunctionType
+ALU = mybir.AluOpType
+
+P = 128
+PACK = 4
+K_PASS = P * PACK
+TOKENS = 256
+TOKEN_TILES = TOKENS // P
+H = 2048
+H_PASSES = H // K_PASS
+H_HALVES = (slice(0, H // 2), slice(H // 2, H))
+R = 512
+I = 7168
+EPS = 1e-05
+BANK = 512
+HALF = 512
+PIECE = 2 * HALF
+BANKS_PER_PIECE = PIECE // BANK
+V_PIECES = H_PASSES * R // PIECE
+U_PIECES = I // PIECE
+RUN = 4
+GATE = 0
+UP = 1
+GATE_VECTOR_COLS = 704
+LOADS_AHEAD = 5
+RAW_SLOTS = 10
+GROUPED_SLOTS = 4
+UP_FIRST_HALF_SLOTS = 2
+UP_SECOND_HALF_SLOTS = 1
+CODE_SLOTS = 4
+ACT_SLOTS = 6
+PRODUCT_SLOTS = 8
+PSUM_BANKS = 8
+
+FLOPS = 2 * TOKENS * (2 * H * R + 2 * R * I)
+
+
+def tile_neuronllamamlp_pa_kernel(
+    tc, x, residual, ln_w, w_gate_v, w_gate_u, w_up_v, w_up_u, out
+):
+    nc = tc.nc
+    x_rows = x.flatten_outer_dims()
+    res_rows = residual.flatten_outer_dims()
+    out_rows = out.flatten_outer_dims()
+    v_views = [w.rearrange("(g p j) r -> p g j r", j=PACK, p=P) for w in (w_gate_v, w_up_v)]
+    u_views = [w.rearrange("(p j) i -> p j i", j=PACK) for w in (w_gate_u, w_up_u)]
+
+    with ExitStack() as ctx:
+        const = ctx.enter_context(tc.tile_pool(name="const", bufs=1))
+        keep = ctx.enter_context(tc.tile_pool(name="keep", bufs=1))
+        small = ctx.enter_context(tc.tile_pool(name="small", bufs=TOKEN_TILES))
+        raw_pool = ctx.enter_context(tc.tile_pool(name="raw", bufs=RAW_SLOTS))
+        grouped_pool = ctx.enter_context(tc.tile_pool(name="grouped", bufs=GROUPED_SLOTS))
+        up_first_pool = ctx.enter_context(tc.tile_pool(name="up_a", bufs=UP_FIRST_HALF_SLOTS))
+        up_second_pool = ctx.enter_context(tc.tile_pool(name="up_b", bufs=UP_SECOND_HALF_SLOTS))
+        u_pool = ctx.enter_context(tc.tile_pool(name="u_codes", bufs=CODE_SLOTS))
+        act_pool = ctx.enter_context(tc.tile_pool(name="gate_act", bufs=ACT_SLOTS))
+        product_pool = ctx.enter_context(tc.tile_pool(name="product", bufs=PRODUCT_SLOTS))
+        psum = ctx.enter_context(tc.psum_pool(name="psum", bufs=PSUM_BANKS))
+        ctx.enter_context(tc.manual_schedule())
+
+
+        n_grouped = keep.tile([P, TOKEN_TILES, H_PASSES, P, PACK], BF16, align_bytes=64)
+        n_codes = keep.tile([P, TOKEN_TILES, H_PASSES, P], U32, align_bytes=64)
+        n_scales = keep.tile([P, TOKEN_TILES, H_PASSES, P], U8, align_bytes=64)
+        v_codes = [
+            keep.tile([P, V_PIECES * PIECE], U32, align_bytes=64, name="v_codes%d" % m)
+            for m in (GATE, UP)
+        ]
+        v_scales = [
+            keep.tile([P, V_PIECES * PIECE], U8, align_bytes=64, name="v_scales%d" % m)
+            for m in (GATE, UP)
+        ]
+        r_grouped = keep.tile([P, 2, TOKEN_TILES, P, PACK], BF16, align_bytes=64)
+        r_codes = keep.tile([P, 2, TOKEN_TILES, P], U32, align_bytes=64)
+        r_scales = keep.tile([P, 2, TOKEN_TILES, P], U8, align_bytes=64)
+
+        x_res, h, h_scaled, sum_sq, rms, rstd, h_t = {}, {}, {}, {}, {}, {}, {}
+        raw, grouped_parts, codes, scales = {}, {}, {}, {}
+        r_t, banks, gate_act = {}, {}, {}
+
+        def load_tokens(tt):
+            rows = slice(tt * P, (tt + 1) * P)
+            x_res[tt] = raw_pool.tile([P, 2, H], BF16, tag="raw", name="x_res")
+            h[tt] = raw_pool.tile([P, H], F32, tag="raw", name="h")
+            h_scaled[tt] = raw_pool.tile([P, H], F32, tag="raw", name="h_scaled")
+            sum_sq[tt] = small.tile([P, 2], F32, name="sum_sq")
+            for cols in H_HALVES:
+                nc.sync.dma_start(out=x_res[tt][:, 0, cols], in_=x_rows[rows, cols])
+                nc.sync.dma_start(out=x_res[tt][:, 1, cols], in_=res_rows[rows, cols])
+
+        def add_and_square(tt, half):
+            cols = H_HALVES[half]
+            nc.vector.tensor_tensor(
+                out=h[tt][:, cols], in0=x_res[tt][:, 0, cols], in1=x_res[tt][:, 1, cols], op=ALU.add
+            )
+            nc.scalar.activation(
+                out=h_scaled[tt][:, cols], in_=h[tt][:, cols], func=ACT.Square,
+                accum_out=sum_sq[tt][:, half : half + 1],
+            )
+
+        def root_mean_square(tt):
+            first_mean = small.tile([P, 1], F32, name="first_mean")
+            nc.scalar.activation(
+                out=first_mean[:], in_=sum_sq[tt][:, 0:1], func=ACT.Identity,
+                scale=1.0 / H, bias=eps[:, 0:1],
+            )
+            rms[tt] = small.tile([P, 1], F32, name="rms")
+            nc.scalar.activation(
+                out=rms[tt][:], in_=sum_sq[tt][:, 1:2], func=ACT.Sqrt,
+                scale=1.0 / H, bias=first_mean[:, 0:1],
+            )
+
+        def reciprocal_rms(tt):
+            rstd[tt] = small.tile([P, 1], F32, name="rstd")
+            nc.vector.reciprocal(rstd[tt][:], rms[tt][:])
+
+        def transpose_tokens(tt):
+            for g in range(H_PASSES):
+                h_t[tt, g] = psum.tile([P, PACK, P], F32, tag="bank", name="h_t")
+                for j in range(PACK):
+                    nc.tensor.transpose(
+                        h_t[tt, g][:, j, :],
+                        h_scaled[tt][:, K_PASS * g + j : K_PASS * (g + 1) : PACK],
+                        ident[:],
+                    )
+
+        def apply_gain(tt):
+            for g in range(H_PASSES):
+                nc.vector.tensor_tensor(
+                    out=n_grouped[:, tt, g, :, :],
+                    in0=h_t[tt, g][:].rearrange("p j t -> p t j"),
+                    in1=gain[:, PACK * g : PACK * (g + 1)].unsqueeze(1).to_broadcast([P, P, PACK]),
+                    op=ALU.mult,
+                )
+
+        def quantise_tokens(tt):
+            nc.vector.quantize_mx(
+                out=n_codes[:, tt].rearrange("p g t -> p (g t)").bitcast(FP8X4),
+                scales=n_scales[:, tt].rearrange("p g t -> p (g t)"),
+                in_=n_grouped[:, tt].rearrange("p g t j -> p (g t j)"),
+            )
+
+        def load_v(m, piece):
+            key = ("v", m, piece)
+            raw[key] = raw_pool.tile([P, PACK, PIECE], BF16, tag="raw", name="raw_v")
+            for half in range(2):
+                nc.sync.dma_start(
+                    out=raw[key][:, :, half * R : (half + 1) * R],
+                    in_=v_views[m][:, 2 * piece + half, :, :],
+                )
+            codes[key] = v_codes[m][:, piece * PIECE : (piece + 1) * PIECE]
+            scales[key] = v_scales[m][:, piece * PIECE : (piece + 1) * PIECE]
+
+        def load_u(piece):
+            if piece < U_PIECES:
+                for m in (GATE, UP):
+                    key = ("u", m, piece)
+                    raw[key] = raw_pool.tile([P, PACK, PIECE], BF16, tag="raw", name="raw_u")
+                    nc.sync.dma_start(
+                        out=raw[key][:], in_=u_views[m][:, :, piece * PIECE : (piece + 1) * PIECE]
+                    )
+
+        def one_grouped_part(key):
+            whole = grouped_pool.tile([P, PIECE, PACK], BF16, align_bytes=64, name="grouped")
+            grouped_parts[key] = [(0, PIECE, whole)]
+
+        def two_grouped_parts(key):
+            first = up_first_pool.tile([P, HALF, PACK], BF16, align_bytes=64, name="up_first")
+            second = up_second_pool.tile([P, HALF, PACK], BF16, align_bytes=64, name="up_second")
+            grouped_parts[key] = [(0, HALF, first), (HALF, PIECE, second)]
+
+        def grouped_columns(key, lo, hi):
+            views = [
+                part[:, lo - start : hi - start, :]
+                for start, end, part in grouped_parts[key]
+                if start <= lo and hi <= end
+            ]
+            return views[0]
+
+        def regroup(copy, key, lo, hi):
+            copy(
+                out=grouped_columns(key, lo, hi).rearrange("p (c i) j -> p c j i", i=RUN),
+                in_=raw[key][:, :, lo:hi].rearrange("p j (c i) -> p c j i", i=RUN),
+            )
+
+        def regroup_first_factor(copy, key):
+            one_grouped_part(key)
+            for half in range(2):
+                cols = slice(half * R, (half + 1) * R)
+                copy(
+                    out=grouped_columns(key, half * R, (half + 1) * R).rearrange(
+                        "p (t m) j -> p m j t", t=PACK
+                    ),
+                    in_=raw[key][:, :, cols].rearrange("p j (m t) -> p m j t", t=PACK),
+                )
+
+        def regroup_on_gpsimd(key, lo, hi):
+            nc.gpsimd.tensor_scalar(
+                out=grouped_columns(key, lo, hi),
+                in0=raw[key][:, :, lo:hi].rearrange("p j c -> p c j"),
+                scalar1=1.0, scalar2=0.0, op0=ALU.mult, op1=ALU.add,
+            )
+
+        def regroup_piece(copy, key):
+            one_grouped_part(key)
+            regroup(copy, key, 0, HALF)
+            regroup(copy, key, HALF, PIECE)
+
+        def quantise_piece(key):
+            if key not in codes:
+                codes[key] = u_pool.tile([P, PIECE], U32, align_bytes=64, name="u_codes")
+                scales[key] = u_pool.tile([P, PIECE], U8, align_bytes=64, name="u_scales")
+            for start, end, part in grouped_parts[key]:
+                nc.vector.quantize_mx(
+                    out=codes[key][:, start:end].bitcast(FP8X4),
+                    scales=scales[key][:, start:end],
+                    in_=part[:].rearrange("p c j -> p (c j)"),
+                )
+
+        def first_product(m, tt):
+            r_t[m, tt] = psum.tile([P, PACK, P], F32, tag="bank", name="r_t")
+            for j in range(PACK):
+                for g in range(H_PASSES):
+                    r_cols = slice(R * g + P * j, R * g + P * (j + 1))
+                    nc.tensor.matmul_mx(
+                        out=r_t[m, tt][:, j, :],
+                        lhsT=v_codes[m][:, r_cols].bitcast(FP8X4),
+                        lhsT_scale=v_scales[m][:, r_cols],
+                        rhs=n_codes[:, tt, g, :].bitcast(FP8X4),
+                        rhs_scale=n_scales[:, tt, g, :],
+                        start=(g == 0),
+                        stop=(g == H_PASSES - 1),
+                    )
+
+        def round_first_product(m, tt):
+            nc.scalar.copy(
+                out=r_grouped[:, m, tt, :, :], in_=r_t[m, tt][:].rearrange("p j t -> p t j")
+            )
+
+        def second_products(piece):
+            for m in (GATE, UP):
+                for tt in range(TOKEN_TILES):
+                    for b in range(BANKS_PER_PIECE):
+                        cols = slice(b * BANK, (b + 1) * BANK)
+                        banks[m, tt, b] = psum.tile([P, BANK], F32, tag="bank", name="bank")
+                        nc.tensor.matmul_mx(
+                            out=banks[m, tt, b][:],
+                            lhsT=r_codes[:, m, tt, :].bitcast(FP8X4),
+                            lhsT_scale=r_scales[:, m, tt, :],
+                            rhs=codes["u", m, piece][:, cols].bitcast(FP8X4),
+                            rhs_scale=scales["u", m, piece][:, cols],
+                            start=True,
+                            stop=True,
+                        )
+
+        def silu_of_gate():
+            for tt in range(TOKEN_TILES):
+                for b in range(BANKS_PER_PIECE):
+                    gate_act[tt, b] = act_pool.tile([P, BANK], F32, name="gate_act")
+                    nc.scalar.activation(
+                        out=gate_act[tt, b][:], in_=banks[GATE, tt, b][:], func=ACT.Silu
+                    )
+
+        def multiply_and_store(piece):
+            for tt in range(TOKEN_TILES):
+                product = product_pool.tile([P, PIECE], F32, name="product")
+                for b in range(BANKS_PER_PIECE):
+                    nc.vector.tensor_tensor(
+                        out=product[:, b * BANK : (b + 1) * BANK],
+                        in0=gate_act[tt, b][:], in1=banks[UP, tt, b][:], op=ALU.mult,
+                    )
+                nc.sync.dma_start(
+                    out=out_rows[tt * P : (tt + 1) * P, piece * PIECE : (piece + 1) * PIECE],
+                    in_=product[:],
+                )
+
+        eps = const.tile([P, 1], F32)
+        nc.vector.memset(eps[:], EPS)
+        warm = const.tile([P, 2], F32)
+        nc.scalar.sqrt(warm[:, 0:1], eps[:])
+        ident = const.tile([P, P], F32)
+        make_identity(nc, ident[:])
+        gain = const.tile([P, H // P], BF16)
+
+        on_vector = nc.vector.tensor_copy
+        on_scalar = nc.scalar.copy
+        load_tokens(0)
+        load_tokens(1)
+        nc.sync.dma_start(
+            out=gain[:].rearrange("p (g j) -> p g j", j=PACK),
+            in_=ln_w.rearrange("(g p j) -> p g j", p=P, j=PACK),
+        )
+        for m in (GATE, UP):
+            for piece in range(V_PIECES):
+                load_v(m, piece)
+        for tt in range(TOKEN_TILES):
+            add_and_square(tt, 0)
+            add_and_square(tt, 1)
+            root_mean_square(tt)
+        load_u(0)
+        load_u(1)
+        reciprocal_rms(0)
+        nc.vector.tensor_scalar_mul(out=h_scaled[0][:], in0=h[0][:], scalar1=rstd[0][:, 0:1])
+        transpose_tokens(0)
+        regroup_first_factor(on_vector, ("v", GATE, 0))
+        reciprocal_rms(1)
+        nc.scalar.activation(out=h_scaled[1][:], in_=h[1][:], func=ACT.Copy, scale=rstd[1][:, 0:1])
+        nc.scalar.activation(out=warm[:, 1:2], in_=eps[:], func=ACT.Silu)
+        transpose_tokens(1)
+        regroup_first_factor(on_vector, ("v", GATE, 1))
+        regroup_first_factor(on_scalar, ("v", UP, 0))
+        apply_gain(0)
+        apply_gain(1)
+        quantise_tokens(0)
+        quantise_tokens(1)
+        quantise_piece(("v", GATE, 0))
+        quantise_piece(("v", GATE, 1))
+        first_product(GATE, 0)
+        first_product(GATE, 1)
+        regroup_first_factor(on_scalar, ("v", UP, 1))
+        load_u(2)
+        load_u(3)
+        quantise_piece(("v", UP, 0))
+        regroup_piece(on_vector, ("u", GATE, 0))
+        quantise_piece(("v", UP, 1))
+        first_product(UP, 0)
+        first_product(UP, 1)
+        round_first_product(GATE, 0)
+        round_first_product(GATE, 1)
+        two_grouped_parts(("u", UP, 0))
+        regroup(on_scalar, ("u", UP, 0), 0, HALF)
+        regroup(on_scalar, ("u", UP, 0), HALF, PIECE)
+        load_u(4)
+        quantise_piece(("u", GATE, 0))
+        regroup_piece(on_vector, ("u", GATE, 1))
+        round_first_product(UP, 0)
+        round_first_product(UP, 1)
+        quantise_piece(("u", UP, 0))
+        nc.vector.quantize_mx(
+            out=r_codes[:].rearrange("p m a t -> p (m a t)").bitcast(FP8X4),
+            scales=r_scales[:].rearrange("p m a t -> p (m a t)"),
+            in_=r_grouped[:].rearrange("p m a t j -> p (m a t j)"),
+        )
+        two_grouped_parts(("u", UP, 1))
+        regroup(on_scalar, ("u", UP, 1), 0, HALF)
+        regroup(on_scalar, ("u", UP, 1), HALF, PIECE)
+
+        for s in range(U_PIECES):
+            load_u(s + LOADS_AHEAD)
+            second_products(s)
+            silu_of_gate()
+            if s + 2 < U_PIECES:
+                one_grouped_part(("u", GATE, s + 2))
+                regroup(on_vector, ("u", GATE, s + 2), 0, GATE_VECTOR_COLS)
+                regroup(on_scalar, ("u", GATE, s + 2), GATE_VECTOR_COLS, PIECE)
+            if s + 1 < U_PIECES:
+                quantise_piece(("u", GATE, s + 1))
+                quantise_piece(("u", UP, s + 1))
+            if s + 2 < U_PIECES:
+                two_grouped_parts(("u", UP, s + 2))
+                regroup(on_scalar, ("u", UP, s + 2), 0, HALF)
+                regroup_on_gpsimd(("u", UP, s + 2), HALF, PIECE)
+            multiply_and_store(s)

@@ -18,7 +18,6 @@ TOKENS = 256
 TOKEN_TILES = TOKENS // P
 H = 2048
 H_PASSES = H // K_PASS
-H_HALVES = (slice(0, H // 2), slice(H // 2, H))
 R = 512
 I = 7168
 EPS = 1e-05
@@ -32,14 +31,14 @@ RUN = 4
 GATE = 0
 UP = 1
 GATE_VECTOR_COLS = 704
-LOADS_AHEAD = 5
-RAW_SLOTS = 10
+GPSIMD_FROM = 640
+LOADS_AHEAD = 4
+RAW_SLOTS = 11
 GROUPED_SLOTS = 4
 UP_FIRST_HALF_SLOTS = 2
 UP_SECOND_HALF_SLOTS = 1
-CODE_SLOTS = 4
-ACT_SLOTS = 6
-PRODUCT_SLOTS = 8
+CODE_SLOTS = 7
+RESULT_SLOTS = 8
 PSUM_BANKS = 8
 
 FLOPS = 2 * TOKENS * (2 * H * R + 2 * R * I)
@@ -63,104 +62,123 @@ def tile_neuronllamamlp_pa_kernel(
         grouped_pool = ctx.enter_context(tc.tile_pool(name="grouped", bufs=GROUPED_SLOTS))
         up_first_pool = ctx.enter_context(tc.tile_pool(name="up_a", bufs=UP_FIRST_HALF_SLOTS))
         up_second_pool = ctx.enter_context(tc.tile_pool(name="up_b", bufs=UP_SECOND_HALF_SLOTS))
-        u_pool = ctx.enter_context(tc.tile_pool(name="u_codes", bufs=CODE_SLOTS))
-        act_pool = ctx.enter_context(tc.tile_pool(name="gate_act", bufs=ACT_SLOTS))
-        product_pool = ctx.enter_context(tc.tile_pool(name="product", bufs=PRODUCT_SLOTS))
+        code_pool = ctx.enter_context(tc.tile_pool(name="codes", bufs=CODE_SLOTS))
+        result_pool = ctx.enter_context(tc.tile_pool(name="result", bufs=RESULT_SLOTS))
         psum = ctx.enter_context(tc.psum_pool(name="psum", bufs=PSUM_BANKS))
         ctx.enter_context(tc.manual_schedule())
 
-
-        n_grouped = keep.tile([P, TOKEN_TILES, H_PASSES, P, PACK], BF16, align_bytes=64)
+        gain = keep.tile([P, H], BF16)
+        junk = keep.tile([P, BANK], BF16)
+        gp_junk = keep.tile([P, 1], F32)
+        n_grouped = keep.tile([P, TOKEN_TILES, H_PASSES * P, PACK], BF16, align_bytes=64)
         n_codes = keep.tile([P, TOKEN_TILES, H_PASSES, P], U32, align_bytes=64)
         n_scales = keep.tile([P, TOKEN_TILES, H_PASSES, P], U8, align_bytes=64)
-        v_codes = [
-            keep.tile([P, V_PIECES * PIECE], U32, align_bytes=64, name="v_codes%d" % m)
-            for m in (GATE, UP)
-        ]
-        v_scales = [
-            keep.tile([P, V_PIECES * PIECE], U8, align_bytes=64, name="v_scales%d" % m)
-            for m in (GATE, UP)
-        ]
         r_grouped = keep.tile([P, 2, TOKEN_TILES, P, PACK], BF16, align_bytes=64)
         r_codes = keep.tile([P, 2, TOKEN_TILES, P], U32, align_bytes=64)
         r_scales = keep.tile([P, 2, TOKEN_TILES, P], U8, align_bytes=64)
 
-        x_res, h, h_scaled, sum_sq, rms, rstd, h_t = {}, {}, {}, {}, {}, {}, {}
+        x_res, h, n, sum_sq, rms, rstd, n_t = {}, {}, {}, {}, {}, {}, {}
         raw, grouped_parts, codes, scales = {}, {}, {}, {}
-        r_t, banks, gate_act = {}, {}, {}
+        r_t, banks, results = {}, {}, {}
 
         def load_tokens(tt):
             rows = slice(tt * P, (tt + 1) * P)
             x_res[tt] = raw_pool.tile([P, 2, H], BF16, tag="raw", name="x_res")
-            h[tt] = raw_pool.tile([P, H], F32, tag="raw", name="h")
-            h_scaled[tt] = raw_pool.tile([P, H], F32, tag="raw", name="h_scaled")
-            sum_sq[tt] = small.tile([P, 2], F32, name="sum_sq")
-            for cols in H_HALVES:
-                nc.sync.dma_start(out=x_res[tt][:, 0, cols], in_=x_rows[rows, cols])
-                nc.sync.dma_start(out=x_res[tt][:, 1, cols], in_=res_rows[rows, cols])
+            nc.sync.dma_start(out=x_res[tt][:, 0, :], in_=x_rows[rows, :])
+            nc.sync.dma_start(out=x_res[tt][:, 1, :], in_=res_rows[rows, :])
 
-        def add_and_square(tt, half):
-            cols = H_HALVES[half]
-            nc.vector.tensor_tensor(
-                out=h[tt][:, cols], in0=x_res[tt][:, 0, cols], in1=x_res[tt][:, 1, cols], op=ALU.add
-            )
-            nc.scalar.activation(
-                out=h_scaled[tt][:, cols], in_=h[tt][:, cols], func=ACT.Square,
-                accum_out=sum_sq[tt][:, half : half + 1],
-            )
+        def spread_gain():
+            for half in range(2):
+                bank = psum.tile([P, 2 * BANK], BF16, tag="bank", name="gain_bank")
+                for b in range(2):
+                    g = 2 * half + b
+                    nc.tensor.matmul(
+                        bank[:, b * BANK : (b + 1) * BANK],
+                        lhsT=ident_bf[:, g : g + 1].to_broadcast([P, P]),
+                        rhs=gain_rows[:],
+                        start=True,
+                        stop=True,
+                    )
+                nc.scalar.copy(out=gain[:, half * 2 * BANK : (half + 1) * 2 * BANK], in_=bank[:])
+
+        def add_tokens(tt):
+            for g in range(H_PASSES):
+                cols = slice(g * BANK, (g + 1) * BANK)
+                h[tt, g] = psum.tile([P, BANK], F32, tag="bank", name="h")
+                for part in range(2):
+                    nc.tensor.matmul(
+                        h[tt, g][:], lhsT=ident_bf[:], rhs=x_res[tt][:, part, cols],
+                        start=(part == 0), stop=(part == 1),
+                    )
+
+        def square_tokens(tt):
+            sum_sq[tt] = small.tile([P, H_PASSES], F32, name="sum_sq")
+            for g in range(H_PASSES):
+                nc.scalar.activation(
+                    out=junk[:], in_=h[tt, g][:], func=ACT.Square,
+                    accum_out=sum_sq[tt][:, g : g + 1],
+                )
 
         def root_mean_square(tt):
-            first_mean = small.tile([P, 1], F32, name="first_mean")
+            scaled = small.tile([P, H_PASSES], F32, name="scaled")
+            mean_sq = small.tile([P, 1], F32, name="mean_sq")
             nc.scalar.activation(
-                out=first_mean[:], in_=sum_sq[tt][:, 0:1], func=ACT.Identity,
-                scale=1.0 / H, bias=eps[:, 0:1],
+                out=scaled[:], in_=sum_sq[tt][:], func=ACT.Copy, scale=1.0 / H,
+                accum_out=mean_sq[:, 0:1],
             )
             rms[tt] = small.tile([P, 1], F32, name="rms")
             nc.scalar.activation(
-                out=rms[tt][:], in_=sum_sq[tt][:, 1:2], func=ACT.Sqrt,
-                scale=1.0 / H, bias=first_mean[:, 0:1],
+                out=rms[tt][:], in_=mean_sq[:, 0:1], func=ACT.Sqrt, bias=eps[:, 0:1]
             )
 
-        def reciprocal_rms(tt):
+        def normalise(tt):
             rstd[tt] = small.tile([P, 1], F32, name="rstd")
             nc.vector.reciprocal(rstd[tt][:], rms[tt][:])
+            n[tt] = result_pool.tile([P, H], BF16, tag="result", name="n")
+            for g in range(H_PASSES):
+                cols = slice(g * BANK, (g + 1) * BANK)
+                nc.vector.scalar_tensor_tensor(
+                    out=n[tt][:, cols], in0=h[tt, g][:], scalar=rstd[tt][:, 0:1],
+                    in1=gain[:, cols], op0=ALU.mult, op1=ALU.mult,
+                )
 
         def transpose_tokens(tt):
-            for g in range(H_PASSES):
-                h_t[tt, g] = psum.tile([P, PACK, P], F32, tag="bank", name="h_t")
-                for j in range(PACK):
-                    nc.tensor.transpose(
-                        h_t[tt, g][:, j, :],
-                        h_scaled[tt][:, K_PASS * g + j : K_PASS * (g + 1) : PACK],
-                        ident[:],
-                    )
+            words = n[tt][:].bitcast(F32)
+            for half in range(2):
+                n_t[tt, half] = psum.tile([P, 2, 2, P], F32, tag="bank", name="n_t")
+                for b in range(2):
+                    g = 2 * half + b
+                    for u in range(2):
+                        nc.tensor.transpose(
+                            n_t[tt, half][:, b, u, :],
+                            words[:, 2 * P * g + u : 2 * P * (g + 1) : 2],
+                            ident[:],
+                        )
 
-        def apply_gain(tt):
-            for g in range(H_PASSES):
-                nc.vector.tensor_tensor(
-                    out=n_grouped[:, tt, g, :, :],
-                    in0=h_t[tt, g][:].rearrange("p j t -> p t j"),
-                    in1=gain[:, PACK * g : PACK * (g + 1)].unsqueeze(1).to_broadcast([P, P, PACK]),
-                    op=ALU.mult,
+        def regroup_tokens(copy, tt):
+            words = n_grouped[:, tt].rearrange("p c j -> p (c j)").bitcast(F32)
+            words = words.rearrange("p (g t u) -> p g t u", g=H_PASSES, u=2)
+            for half in range(2):
+                copy(
+                    out=words[:, 2 * half : 2 * half + 2],
+                    in_=n_t[tt, half][:].rearrange("p g u t -> p g t u"),
                 )
 
         def quantise_tokens(tt):
             nc.vector.quantize_mx(
                 out=n_codes[:, tt].rearrange("p g t -> p (g t)").bitcast(FP8X4),
                 scales=n_scales[:, tt].rearrange("p g t -> p (g t)"),
-                in_=n_grouped[:, tt].rearrange("p g t j -> p (g t j)"),
+                in_=n_grouped[:, tt].rearrange("p c j -> p (c j)"),
             )
 
-        def load_v(m, piece):
-            key = ("v", m, piece)
-            raw[key] = raw_pool.tile([P, PACK, PIECE], BF16, tag="raw", name="raw_v")
-            for half in range(2):
-                nc.sync.dma_start(
-                    out=raw[key][:, :, half * R : (half + 1) * R],
-                    in_=v_views[m][:, 2 * piece + half, :, :],
-                )
-            codes[key] = v_codes[m][:, piece * PIECE : (piece + 1) * PIECE]
-            scales[key] = v_scales[m][:, piece * PIECE : (piece + 1) * PIECE]
+        def load_v(m, g):
+            key = ("v", m, g // 2)
+            half = g % 2
+            if half == 0:
+                raw[key] = raw_pool.tile([P, PACK, PIECE], BF16, tag="raw", name="raw_v")
+            nc.sync.dma_start(
+                out=raw[key][:, :, half * R : (half + 1) * R], in_=v_views[m][:, g, :, :]
+            )
 
         def load_u(piece):
             if piece < U_PIECES:
@@ -194,16 +212,18 @@ def tile_neuronllamamlp_pa_kernel(
                 in_=raw[key][:, :, lo:hi].rearrange("p j (c i) -> p c j i", i=RUN),
             )
 
-        def regroup_first_factor(copy, key):
-            one_grouped_part(key)
-            for half in range(2):
-                cols = slice(half * R, (half + 1) * R)
-                copy(
-                    out=grouped_columns(key, half * R, (half + 1) * R).rearrange(
-                        "p (t m) j -> p m j t", t=PACK
-                    ),
-                    in_=raw[key][:, :, cols].rearrange("p j (m t) -> p m j t", t=PACK),
-                )
+        def regroup_v(copy, m, g, lo=0, hi=R):
+            key = ("v", m, g // 2)
+            if key not in grouped_parts:
+                one_grouped_part(key)
+            start = (g % 2) * R
+            grouped = grouped_columns(key, start, start + R)
+            copy(
+                out=grouped.rearrange("p (t m) j -> p m j t", t=PACK)[:, lo // PACK : hi // PACK],
+                in_=raw[key][:, :, start + lo : start + hi].rearrange(
+                    "p j (m t) -> p m j t", t=PACK
+                ),
+            )
 
         def regroup_on_gpsimd(key, lo, hi):
             nc.gpsimd.tensor_scalar(
@@ -212,15 +232,28 @@ def tile_neuronllamamlp_pa_kernel(
                 scalar1=1.0, scalar2=0.0, op0=ALU.mult, op1=ALU.add,
             )
 
-        def regroup_piece(copy, key):
-            one_grouped_part(key)
-            regroup(copy, key, 0, HALF)
-            regroup(copy, key, HALF, PIECE)
+        def regroup_v_on_gpsimd(m, g, lo, hi):
+            key = ("v", m, g // 2)
+            if key not in grouped_parts:
+                one_grouped_part(key)
+            start = (g % 2) * R
+            grouped = grouped_columns(key, start, start + R)
+            nc.gpsimd.tensor_scalar(
+                out=grouped.rearrange("p (t m) j -> p m j t", t=PACK)[:, lo // PACK : hi // PACK],
+                in0=raw[key][:, :, start + lo : start + hi].rearrange(
+                    "p j (m t) -> p m j t", t=PACK
+                ),
+                scalar1=1.0, scalar2=0.0, op0=ALU.mult, op1=ALU.add,
+            )
+
+        def gpsimd_waits_for_rstd(tt):
+            nc.gpsimd.tensor_scalar(
+                out=gp_junk[:], in0=rstd[tt][:], scalar1=1.0, scalar2=0.0, op0=ALU.mult, op1=ALU.add,
+            )
 
         def quantise_piece(key):
-            if key not in codes:
-                codes[key] = u_pool.tile([P, PIECE], U32, align_bytes=64, name="u_codes")
-                scales[key] = u_pool.tile([P, PIECE], U8, align_bytes=64, name="u_scales")
+            codes[key] = code_pool.tile([P, PIECE], U32, align_bytes=64, name="codes")
+            scales[key] = code_pool.tile([P, PIECE], U8, align_bytes=64, name="scales")
             for start, end, part in grouped_parts[key]:
                 nc.vector.quantize_mx(
                     out=codes[key][:, start:end].bitcast(FP8X4),
@@ -232,20 +265,28 @@ def tile_neuronllamamlp_pa_kernel(
             r_t[m, tt] = psum.tile([P, PACK, P], F32, tag="bank", name="r_t")
             for j in range(PACK):
                 for g in range(H_PASSES):
-                    r_cols = slice(R * g + P * j, R * g + P * (j + 1))
+                    key = ("v", m, g // 2)
+                    r_cols = slice(R * (g % 2) + P * j, R * (g % 2) + P * (j + 1))
                     nc.tensor.matmul_mx(
                         out=r_t[m, tt][:, j, :],
-                        lhsT=v_codes[m][:, r_cols].bitcast(FP8X4),
-                        lhsT_scale=v_scales[m][:, r_cols],
+                        lhsT=codes[key][:, r_cols].bitcast(FP8X4),
+                        lhsT_scale=scales[key][:, r_cols],
                         rhs=n_codes[:, tt, g, :].bitcast(FP8X4),
                         rhs_scale=n_scales[:, tt, g, :],
                         start=(g == 0),
                         stop=(g == H_PASSES - 1),
                     )
 
-        def round_first_product(m, tt):
-            nc.scalar.copy(
+        def round_first_product(copy, m, tt):
+            copy(
                 out=r_grouped[:, m, tt, :, :], in_=r_t[m, tt][:].rearrange("p j t -> p t j")
+            )
+
+        def quantise_first_products():
+            nc.vector.quantize_mx(
+                out=r_codes[:].rearrange("p m a t -> p (m a t)").bitcast(FP8X4),
+                scales=r_scales[:].rearrange("p m a t -> p (m a t)"),
+                in_=r_grouped[:].rearrange("p m a t j -> p (m a t j)"),
             )
 
         def second_products(piece):
@@ -266,95 +307,112 @@ def tile_neuronllamamlp_pa_kernel(
 
         def silu_of_gate():
             for tt in range(TOKEN_TILES):
+                results[tt] = result_pool.tile([P, PIECE], F32, tag="result", name="result")
                 for b in range(BANKS_PER_PIECE):
-                    gate_act[tt, b] = act_pool.tile([P, BANK], F32, name="gate_act")
                     nc.scalar.activation(
-                        out=gate_act[tt, b][:], in_=banks[GATE, tt, b][:], func=ACT.Silu
+                        out=results[tt][:, b * BANK : (b + 1) * BANK],
+                        in_=banks[GATE, tt, b][:], func=ACT.Silu,
                     )
 
-        def multiply_and_store(piece):
+        def multiply_and_store(piece, columns_per_store):
             for tt in range(TOKEN_TILES):
-                product = product_pool.tile([P, PIECE], F32, name="product")
                 for b in range(BANKS_PER_PIECE):
+                    cols = slice(b * BANK, (b + 1) * BANK)
                     nc.vector.tensor_tensor(
-                        out=product[:, b * BANK : (b + 1) * BANK],
-                        in0=gate_act[tt, b][:], in1=banks[UP, tt, b][:], op=ALU.mult,
+                        out=results[tt][:, cols], in0=results[tt][:, cols],
+                        in1=banks[UP, tt, b][:], op=ALU.mult,
                     )
-                nc.sync.dma_start(
-                    out=out_rows[tt * P : (tt + 1) * P, piece * PIECE : (piece + 1) * PIECE],
-                    in_=product[:],
-                )
+                    done = (b + 1) * BANK
+                    if done % columns_per_store == 0:
+                        nc.sync.dma_start(
+                            out=out_rows[
+                                tt * P : (tt + 1) * P,
+                                piece * PIECE + done - columns_per_store : piece * PIECE + done,
+                            ],
+                            in_=results[tt][:, done - columns_per_store : done],
+                        )
 
+        on_vector = nc.vector.tensor_copy
+        on_scalar = nc.scalar.copy
+
+        gain_rows = const.tile([P, BANK], BF16)
+        nc.vector.memset(gain_rows[:], 0.0)
+        nc.scalar.dma_start(
+            out=gain_rows[0:H_PASSES, :], in_=ln_w.rearrange("(g c) -> g c", c=BANK)
+        )
         eps = const.tile([P, 1], F32)
         nc.vector.memset(eps[:], EPS)
         warm = const.tile([P, 2], F32)
         nc.scalar.sqrt(warm[:, 0:1], eps[:])
+        ident_bf = const.tile([P, P], BF16)
+        make_identity(nc, ident_bf[:])
         ident = const.tile([P, P], F32)
         make_identity(nc, ident[:])
-        gain = const.tile([P, H // P], BF16)
 
-        on_vector = nc.vector.tensor_copy
-        on_scalar = nc.scalar.copy
+        load_v(GATE, 0)
+        load_v(GATE, 1)
         load_tokens(0)
+        load_v(GATE, 2)
+        load_v(GATE, 3)
         load_tokens(1)
-        nc.sync.dma_start(
-            out=gain[:].rearrange("p (g j) -> p g j", j=PACK),
-            in_=ln_w.rearrange("(g p j) -> p g j", p=P, j=PACK),
-        )
-        for m in (GATE, UP):
-            for piece in range(V_PIECES):
-                load_v(m, piece)
-        for tt in range(TOKEN_TILES):
-            add_and_square(tt, 0)
-            add_and_square(tt, 1)
-            root_mean_square(tt)
-        load_u(0)
-        load_u(1)
-        reciprocal_rms(0)
-        nc.vector.tensor_scalar_mul(out=h_scaled[0][:], in0=h[0][:], scalar1=rstd[0][:, 0:1])
-        transpose_tokens(0)
-        regroup_first_factor(on_vector, ("v", GATE, 0))
-        reciprocal_rms(1)
-        nc.scalar.activation(out=h_scaled[1][:], in_=h[1][:], func=ACT.Copy, scale=rstd[1][:, 0:1])
-        nc.scalar.activation(out=warm[:, 1:2], in_=eps[:], func=ACT.Silu)
-        transpose_tokens(1)
-        regroup_first_factor(on_vector, ("v", GATE, 1))
-        regroup_first_factor(on_scalar, ("v", UP, 0))
-        apply_gain(0)
-        apply_gain(1)
-        quantise_tokens(0)
-        quantise_tokens(1)
+        for g in range(H_PASSES):
+            load_v(UP, g)
+        for piece in range(LOADS_AHEAD):
+            load_u(piece)
+        spread_gain()
+        regroup_v(on_vector, GATE, 0)
+        regroup_v(on_vector, GATE, 1, 0, HALF // 2)
+        regroup_v(on_scalar, GATE, 1, HALF // 2, HALF)
+        add_tokens(0)
+        square_tokens(0)
+        root_mean_square(0)
         quantise_piece(("v", GATE, 0))
+        regroup_v(on_vector, GATE, 2)
+        regroup_v(on_vector, GATE, 3, 0, HALF // 2)
+        add_tokens(1)
+        square_tokens(1)
+        root_mean_square(1)
+        normalise(0)
+        gpsimd_waits_for_rstd(0)
+        regroup_v_on_gpsimd(GATE, 3, HALF // 2, HALF)
+        transpose_tokens(0)
         quantise_piece(("v", GATE, 1))
+        regroup_v(on_vector, UP, 0)
+        nc.scalar.activation(out=warm[:, 1:2], in_=eps[:], func=ACT.Silu)
+        regroup_tokens(on_scalar, 0)
+        normalise(1)
+        gpsimd_waits_for_rstd(1)
+        regroup_v_on_gpsimd(UP, 2, 0, 384)
+        transpose_tokens(1)
+        quantise_tokens(0)
         first_product(GATE, 0)
-        first_product(GATE, 1)
-        regroup_first_factor(on_scalar, ("v", UP, 1))
-        load_u(2)
-        load_u(3)
+        regroup_v(on_scalar, UP, 1)
+        regroup_tokens(on_scalar, 1)
+        regroup_v(on_vector, UP, 2, 384, HALF)
+        regroup_v(on_vector, UP, 3)
         quantise_piece(("v", UP, 0))
-        regroup_piece(on_vector, ("u", GATE, 0))
+        quantise_tokens(1)
+        first_product(GATE, 1)
+        two_grouped_parts(("u", UP, 0))
+        regroup(on_scalar, ("u", UP, 0), 0, HALF)
         quantise_piece(("v", UP, 1))
         first_product(UP, 0)
         first_product(UP, 1)
-        round_first_product(GATE, 0)
-        round_first_product(GATE, 1)
-        two_grouped_parts(("u", UP, 0))
-        regroup(on_scalar, ("u", UP, 0), 0, HALF)
+        one_grouped_part(("u", GATE, 0))
+        regroup(on_vector, ("u", GATE, 0), 0, PIECE)
+        round_first_product(on_scalar, GATE, 0)
+        round_first_product(on_scalar, GATE, 1)
         regroup(on_scalar, ("u", UP, 0), HALF, PIECE)
-        load_u(4)
         quantise_piece(("u", GATE, 0))
-        regroup_piece(on_vector, ("u", GATE, 1))
-        round_first_product(UP, 0)
-        round_first_product(UP, 1)
+        round_first_product(on_scalar, UP, 0)
+        round_first_product(on_scalar, UP, 1)
         quantise_piece(("u", UP, 0))
-        nc.vector.quantize_mx(
-            out=r_codes[:].rearrange("p m a t -> p (m a t)").bitcast(FP8X4),
-            scales=r_scales[:].rearrange("p m a t -> p (m a t)"),
-            in_=r_grouped[:].rearrange("p m a t j -> p (m a t j)"),
-        )
+        quantise_first_products()
+        one_grouped_part(("u", GATE, 1))
+        regroup(on_vector, ("u", GATE, 1), 0, PIECE)
         two_grouped_parts(("u", UP, 1))
         regroup(on_scalar, ("u", UP, 1), 0, HALF)
-        regroup(on_scalar, ("u", UP, 1), HALF, PIECE)
+        regroup(on_vector, ("u", UP, 1), HALF, PIECE)
 
         for s in range(U_PIECES):
             load_u(s + LOADS_AHEAD)
@@ -370,5 +428,6 @@ def tile_neuronllamamlp_pa_kernel(
             if s + 2 < U_PIECES:
                 two_grouped_parts(("u", UP, s + 2))
                 regroup(on_scalar, ("u", UP, s + 2), 0, HALF)
-                regroup_on_gpsimd(("u", UP, s + 2), HALF, PIECE)
-            multiply_and_store(s)
+                regroup(on_scalar, ("u", UP, s + 2), HALF, GPSIMD_FROM)
+                regroup_on_gpsimd(("u", UP, s + 2), GPSIMD_FROM, PIECE)
+            multiply_and_store(s, PIECE if s + 1 < U_PIECES else BANK)

@@ -239,9 +239,11 @@ def tile_neuronllamamlp_pa_kernel(
             start = (g % 2) * R
             grouped = grouped_columns(key, start, start + R)
             nc.gpsimd.tensor_scalar(
-                out=grouped.rearrange("p (t m) j -> p m j t", t=PACK)[:, lo // PACK : hi // PACK],
+                out=grouped.rearrange("p (t m) j -> p t m j", t=PACK)[
+                    :, :, lo // PACK : hi // PACK
+                ],
                 in0=raw[key][:, :, start + lo : start + hi].rearrange(
-                    "p j (m t) -> p m j t", t=PACK
+                    "p j (m t) -> p t m j", t=PACK
                 ),
                 scalar1=1.0, scalar2=0.0, op0=ALU.mult, op1=ALU.add,
             )
@@ -337,7 +339,7 @@ def tile_neuronllamamlp_pa_kernel(
 
         gain_rows = const.tile([P, BANK], BF16)
         nc.vector.memset(gain_rows[:], 0.0)
-        nc.scalar.dma_start(
+        nc.sync.dma_start(
             out=gain_rows[0:H_PASSES, :], in_=ln_w.rearrange("(g c) -> g c", c=BANK)
         )
         eps = const.tile([P, 1], F32)

@@ -173,12 +173,9 @@ def tile_neuronllamamlp_pa_kernel(
 
         def load_v(m, g):
             key = ("v", m, g // 2)
-            half = g % 2
-            if half == 0:
-                raw[key] = raw_pool.tile([P, PACK, PIECE], BF16, tag="raw", name="raw_v")
-            nc.sync.dma_start(
-                out=raw[key][:, :, half * R : (half + 1) * R], in_=v_views[m][:, g, :, :]
-            )
+            if g % 2 == 0:
+                raw[key] = raw_pool.tile([P, 2, PACK, R], BF16, tag="raw", name="raw_v")
+            nc.sync.dma_start(out=raw[key][:, g % 2, :, :], in_=v_views[m][:, g, :, :])
 
         def load_u(piece):
             if piece < U_PIECES:
@@ -212,39 +209,34 @@ def tile_neuronllamamlp_pa_kernel(
                 in_=raw[key][:, :, lo:hi].rearrange("p j (c i) -> p c j i", i=RUN),
             )
 
-        def regroup_v(copy, m, g, lo=0, hi=R):
+        def first_factor_views(m, g, t0, t1):
             key = ("v", m, g // 2)
             if key not in grouped_parts:
                 one_grouped_part(key)
             start = (g % 2) * R
-            grouped = grouped_columns(key, start, start + R)
+            grouped = grouped_columns(key, start + P * t0, start + P * t1)
+            rows = raw[key][:, g % 2, :, :].rearrange("p j (m t) -> p j m t", t=PACK)
+            return grouped.rearrange("p (t m) j -> p t m j", m=P), rows[:, :, :, t0:t1]
+
+        def regroup_v(copy, m, g, t0=0, t1=PACK):
+            grouped, rows = first_factor_views(m, g, t0, t1)
             copy(
-                out=grouped.rearrange("p (t m) j -> p m j t", t=PACK)[:, lo // PACK : hi // PACK],
-                in_=raw[key][:, :, start + lo : start + hi].rearrange(
-                    "p j (m t) -> p m j t", t=PACK
-                ),
+                out=grouped.rearrange("p t m j -> p m j t"),
+                in_=rows.rearrange("p j m t -> p m j t"),
+            )
+
+        def regroup_v_on_gpsimd(m, g, t0, t1):
+            grouped, rows = first_factor_views(m, g, t0, t1)
+            nc.gpsimd.tensor_scalar(
+                out=grouped,
+                in0=rows.rearrange("p j m t -> p t m j"),
+                scalar1=1.0, scalar2=0.0, op0=ALU.mult, op1=ALU.add,
             )
 
         def regroup_on_gpsimd(key, lo, hi):
             nc.gpsimd.tensor_scalar(
                 out=grouped_columns(key, lo, hi),
                 in0=raw[key][:, :, lo:hi].rearrange("p j c -> p c j"),
-                scalar1=1.0, scalar2=0.0, op0=ALU.mult, op1=ALU.add,
-            )
-
-        def regroup_v_on_gpsimd(m, g, lo, hi):
-            key = ("v", m, g // 2)
-            if key not in grouped_parts:
-                one_grouped_part(key)
-            start = (g % 2) * R
-            grouped = grouped_columns(key, start, start + R)
-            nc.gpsimd.tensor_scalar(
-                out=grouped.rearrange("p (t m) j -> p t m j", t=PACK)[
-                    :, :, lo // PACK : hi // PACK
-                ],
-                in0=raw[key][:, :, start + lo : start + hi].rearrange(
-                    "p j (m t) -> p t m j", t=PACK
-                ),
                 scalar1=1.0, scalar2=0.0, op0=ALU.mult, op1=ALU.add,
             )
 
@@ -339,9 +331,6 @@ def tile_neuronllamamlp_pa_kernel(
 
         gain_rows = const.tile([P, BANK], BF16)
         nc.vector.memset(gain_rows[:], 0.0)
-        nc.sync.dma_start(
-            out=gain_rows[0:H_PASSES, :], in_=ln_w.rearrange("(g c) -> g c", c=BANK)
-        )
         eps = const.tile([P, 1], F32)
         nc.vector.memset(eps[:], EPS)
         warm = const.tile([P, 2], F32)
@@ -353,6 +342,9 @@ def tile_neuronllamamlp_pa_kernel(
 
         load_v(GATE, 0)
         load_v(GATE, 1)
+        nc.sync.dma_start(
+            out=gain_rows[0:H_PASSES, :], in_=ln_w.rearrange("(g c) -> g c", c=BANK)
+        )
         load_tokens(0)
         load_v(GATE, 2)
         load_v(GATE, 3)
@@ -361,22 +353,22 @@ def tile_neuronllamamlp_pa_kernel(
             load_v(UP, g)
         for piece in range(LOADS_AHEAD):
             load_u(piece)
-        spread_gain()
         regroup_v(on_vector, GATE, 0)
-        regroup_v(on_vector, GATE, 1, 0, HALF // 2)
-        regroup_v(on_scalar, GATE, 1, HALF // 2, HALF)
+        regroup_v(on_vector, GATE, 1, 0, 2)
+        regroup_v(on_scalar, GATE, 1, 2, PACK)
+        spread_gain()
         add_tokens(0)
         square_tokens(0)
         root_mean_square(0)
         quantise_piece(("v", GATE, 0))
         regroup_v(on_vector, GATE, 2)
-        regroup_v(on_vector, GATE, 3, 0, HALF // 2)
+        regroup_v(on_vector, GATE, 3, 0, 2)
         add_tokens(1)
         square_tokens(1)
         root_mean_square(1)
         normalise(0)
         gpsimd_waits_for_rstd(0)
-        regroup_v_on_gpsimd(GATE, 3, HALF // 2, HALF)
+        regroup_v_on_gpsimd(GATE, 3, 2, PACK)
         transpose_tokens(0)
         quantise_piece(("v", GATE, 1))
         regroup_v(on_vector, UP, 0)
@@ -384,13 +376,13 @@ def tile_neuronllamamlp_pa_kernel(
         regroup_tokens(on_scalar, 0)
         normalise(1)
         gpsimd_waits_for_rstd(1)
-        regroup_v_on_gpsimd(UP, 2, 0, 384)
+        regroup_v_on_gpsimd(UP, 2, 0, 3)
         transpose_tokens(1)
         quantise_tokens(0)
         first_product(GATE, 0)
         regroup_v(on_scalar, UP, 1)
         regroup_tokens(on_scalar, 1)
-        regroup_v(on_vector, UP, 2, 384, HALF)
+        regroup_v(on_vector, UP, 2, 3, PACK)
         regroup_v(on_vector, UP, 3)
         quantise_piece(("v", UP, 0))
         quantise_tokens(1)

@@ -221,8 +221,8 @@ def tile_neuronllamamlp_pa_kernel(
         def regroup_v(copy, m, g, t0=0, t1=PACK):
             grouped, rows = first_factor_views(m, g, t0, t1)
             copy(
-                out=grouped.rearrange("p t m j -> p m j t"),
-                in_=rows.rearrange("p j m t -> p m j t"),
+                out=grouped.rearrange("p t (m i) j -> p t m j i", i=2),
+                in_=rows.rearrange("p j (m i) t -> p t m j i", i=2),
             )
 
         def regroup_v_on_gpsimd(m, g, t0, t1):

@@ -30,7 +30,7 @@ U_PIECES = I // PIECE
 RUN = 4
 GATE = 0
 UP = 1
-GATE_VECTOR_COLS = 704
+GATE_VECTOR_COLS = 608
 GPSIMD_FROM = 640
 LOADS_AHEAD = 4
 RAW_SLOTS = 11

@@ -30,7 +30,8 @@ U_PIECES = I // PIECE
 RUN = 4
 GATE = 0
 UP = 1
-GATE_VECTOR_COLS = 608
+GATE_VECTOR_COLS = 576
+TENSOR_COLS = 224
 GPSIMD_FROM = 640
 LOADS_AHEAD = 4
 RAW_SLOTS = 11
@@ -233,6 +234,17 @@ def tile_neuronllamamlp_pa_kernel(
                 scalar1=1.0, scalar2=0.0, op0=ALU.mult, op1=ALU.add,
             )
 
+        def regroup_through_psum(key, lo, hi):
+            bank = psum.tile([P, hi - lo, PACK], BF16, tag="bank", name="grouped_bank")
+            middle = (lo + hi) // 2
+            for c0, c1 in ((lo, middle), (middle, hi)):
+                nc.tensor.matmul(
+                    bank[:, c0 - lo : c1 - lo, :], lhsT=ident_bf[:],
+                    rhs=raw[key][:, :, c0:c1].rearrange("p j c -> p c j"),
+                    start=True, stop=True,
+                )
+            nc.scalar.copy(out=grouped_columns(key, lo, hi), in_=bank[:])
+
         def regroup_on_gpsimd(key, lo, hi):
             nc.gpsimd.tensor_scalar(
                 out=grouped_columns(key, lo, hi),
@@ -400,10 +412,11 @@ def tile_neuronllamamlp_pa_kernel(
         quantise_piece(("u", GATE, 0))
         round_first_product(on_scalar, UP, 0)
         round_first_product(on_scalar, UP, 1)
+        one_grouped_part(("u", GATE, 1))
+        regroup(on_vector, ("u", GATE, 1), 0, HALF)
         quantise_piece(("u", UP, 0))
         quantise_first_products()
-        one_grouped_part(("u", GATE, 1))
-        regroup(on_vector, ("u", GATE, 1), 0, PIECE)
+        regroup(on_vector, ("u", GATE, 1), HALF, PIECE)
         two_grouped_parts(("u", UP, 1))
         regroup(on_scalar, ("u", UP, 1), 0, HALF)
         regroup(on_vector, ("u", UP, 1), HALF, PIECE)
@@ -421,7 +434,8 @@ def tile_neuronllamamlp_pa_kernel(
                 quantise_piece(("u", UP, s + 1))
             if s + 2 < U_PIECES:
                 two_grouped_parts(("u", UP, s + 2))
-                regroup(on_scalar, ("u", UP, s + 2), 0, HALF)
+                regroup_through_psum(("u", UP, s + 2), 0, TENSOR_COLS)
+                regroup(on_scalar, ("u", UP, s + 2), TENSOR_COLS, HALF)
                 regroup(on_scalar, ("u", UP, s + 2), HALF, GPSIMD_FROM)
                 regroup_on_gpsimd(("u", UP, s + 2), GPSIMD_FROM, PIECE)
             multiply_and_store(s, PIECE if s + 1 < U_PIECES else BANK)

@@ -18,6 +18,7 @@ TOKENS = 256
 TOKEN_TILES = TOKENS // P
 H = 2048
 H_PASSES = H // K_PASS
+GAIN_ROWS = H // P
 R = 512
 I = 7168
 EPS = 1e-05
@@ -30,11 +31,10 @@ U_PIECES = I // PIECE
 RUN = 4
 GATE = 0
 UP = 1
-GATE_VECTOR_COLS = 576
+GATE_VECTOR_COLS = 640
 TENSOR_COLS = 224
 GPSIMD_FROM = 640
-LOADS_AHEAD = 4
-RAW_SLOTS = 11
+RAW_SLOTS = 12
 GROUPED_SLOTS = 4
 UP_FIRST_HALF_SLOTS = 2
 UP_SECOND_HALF_SLOTS = 1
@@ -69,6 +69,7 @@ def tile_neuronllamamlp_pa_kernel(
         ctx.enter_context(tc.manual_schedule())
 
         gain = keep.tile([P, H], BF16)
+        gain_cols = keep.tile([P, GAIN_ROWS], BF16)
         junk = keep.tile([P, BANK], BF16)
         gp_junk = keep.tile([P, 1], F32)
         n_grouped = keep.tile([P, TOKEN_TILES, H_PASSES * P, PACK], BF16, align_bytes=64)
@@ -88,19 +89,21 @@ def tile_neuronllamamlp_pa_kernel(
             nc.sync.dma_start(out=x_res[tt][:, 0, :], in_=x_rows[rows, :])
             nc.sync.dma_start(out=x_res[tt][:, 1, :], in_=res_rows[rows, :])
 
-        def spread_gain():
-            for half in range(2):
-                bank = psum.tile([P, 2 * BANK], BF16, tag="bank", name="gain_bank")
-                for b in range(2):
-                    g = 2 * half + b
-                    nc.tensor.matmul(
-                        bank[:, b * BANK : (b + 1) * BANK],
-                        lhsT=ident_bf[:, g : g + 1].to_broadcast([P, P]),
-                        rhs=gain_rows[:],
-                        start=True,
-                        stop=True,
-                    )
-                nc.scalar.copy(out=gain[:, half * 2 * BANK : (half + 1) * 2 * BANK], in_=bank[:])
+        def turn_gain(copy):
+            columns = psum.tile([P, P], BF16, tag="bank", name="gain_columns")
+            nc.tensor.transpose(columns[:], gain_rows[:], ident_bf[:])
+            copy(out=gain_cols[:], in_=columns[:, 0:GAIN_ROWS])
+
+        def spread_gain(copy, half):
+            bank = psum.tile([P, 2 * BANK], BF16, tag="bank", name="gain_bank")
+            for i in range(GAIN_ROWS // 2):
+                g = half * (GAIN_ROWS // 2) + i
+                nc.tensor.transpose(
+                    bank[:, i * P : (i + 1) * P],
+                    gain_cols[:, g : g + 1].to_broadcast([P, P]),
+                    ident_bf[:],
+                )
+            copy(out=gain[:, half * 2 * BANK : (half + 1) * 2 * BANK], in_=bank[:])
 
         def add_tokens(tt):
             for g in range(H_PASSES):
@@ -179,22 +182,24 @@ def tile_neuronllamamlp_pa_kernel(
             nc.sync.dma_start(out=raw[key][:, g % 2, :, :], in_=v_views[m][:, g, :, :])
 
         def load_u(piece):
-            if piece < U_PIECES:
-                for m in (GATE, UP):
-                    key = ("u", m, piece)
-                    raw[key] = raw_pool.tile([P, PACK, PIECE], BF16, tag="raw", name="raw_u")
-                    nc.sync.dma_start(
-                        out=raw[key][:], in_=u_views[m][:, :, piece * PIECE : (piece + 1) * PIECE]
-                    )
+            for m in (GATE, UP):
+                key = ("u", m, piece)
+                raw[key] = raw_pool.tile([P, PACK, PIECE], BF16, tag="raw", name="raw_u")
+                nc.sync.dma_start(
+                    out=raw[key][:], in_=u_views[m][:, :, piece * PIECE : (piece + 1) * PIECE]
+                )
 
         def one_grouped_part(key):
             whole = grouped_pool.tile([P, PIECE, PACK], BF16, align_bytes=64, name="grouped")
             grouped_parts[key] = [(0, PIECE, whole)]
 
-        def two_grouped_parts(key):
+        def first_grouped_part(key):
             first = up_first_pool.tile([P, HALF, PACK], BF16, align_bytes=64, name="up_first")
+            grouped_parts[key] = [(0, HALF, first)]
+
+        def second_grouped_part(key):
             second = up_second_pool.tile([P, HALF, PACK], BF16, align_bytes=64, name="up_second")
-            grouped_parts[key] = [(0, HALF, first), (HALF, PIECE, second)]
+            grouped_parts[key].append((HALF, PIECE, second))
 
         def grouped_columns(key, lo, hi):
             views = [
@@ -257,15 +262,15 @@ def tile_neuronllamamlp_pa_kernel(
                 out=gp_junk[:], in0=rstd[tt][:], scalar1=1.0, scalar2=0.0, op0=ALU.mult, op1=ALU.add,
             )
 
-        def quantise_piece(key):
-            codes[key] = code_pool.tile([P, PIECE], U32, align_bytes=64, name="codes")
-            scales[key] = code_pool.tile([P, PIECE], U8, align_bytes=64, name="scales")
-            for start, end, part in grouped_parts[key]:
-                nc.vector.quantize_mx(
-                    out=codes[key][:, start:end].bitcast(FP8X4),
-                    scales=scales[key][:, start:end],
-                    in_=part[:].rearrange("p c j -> p (c j)"),
-                )
+        def quantise(key, lo, hi):
+            if key not in codes:
+                codes[key] = code_pool.tile([P, PIECE], U32, align_bytes=64, name="codes")
+                scales[key] = code_pool.tile([P, PIECE], U8, align_bytes=64, name="scales")
+            nc.vector.quantize_mx(
+                out=codes[key][:, lo:hi].bitcast(FP8X4),
+                scales=scales[key][:, lo:hi],
+                in_=grouped_columns(key, lo, hi).rearrange("p c j -> p (c j)"),
+            )
 
         def first_product(m, tt):
             r_t[m, tt] = psum.tile([P, PACK, P], F32, tag="bank", name="r_t")
@@ -295,21 +300,18 @@ def tile_neuronllamamlp_pa_kernel(
                 in_=r_grouped[:].rearrange("p m a t j -> p (m a t j)"),
             )
 
-        def second_products(piece):
-            for m in (GATE, UP):
-                for tt in range(TOKEN_TILES):
-                    for b in range(BANKS_PER_PIECE):
-                        cols = slice(b * BANK, (b + 1) * BANK)
-                        banks[m, tt, b] = psum.tile([P, BANK], F32, tag="bank", name="bank")
-                        nc.tensor.matmul_mx(
-                            out=banks[m, tt, b][:],
-                            lhsT=r_codes[:, m, tt, :].bitcast(FP8X4),
-                            lhsT_scale=r_scales[:, m, tt, :],
-                            rhs=codes["u", m, piece][:, cols].bitcast(FP8X4),
-                            rhs_scale=scales["u", m, piece][:, cols],
-                            start=True,
-                            stop=True,
-                        )
+        def second_product(m, piece, tt, b):
+            cols = slice(b * BANK, (b + 1) * BANK)
+            banks[m, tt, b] = psum.tile([P, BANK], F32, tag="bank", name="bank")
+            nc.tensor.matmul_mx(
+                out=banks[m, tt, b][:],
+                lhsT=r_codes[:, m, tt, :].bitcast(FP8X4),
+                lhsT_scale=r_scales[:, m, tt, :],
+                rhs=codes["u", m, piece][:, cols].bitcast(FP8X4),
+                rhs_scale=scales["u", m, piece][:, cols],
+                start=True,
+                stop=True,
+            )
 
         def silu_of_gate():
             for tt in range(TOKEN_TILES):
@@ -320,9 +322,15 @@ def tile_neuronllamamlp_pa_kernel(
                         in_=banks[GATE, tt, b][:], func=ACT.Silu,
                     )
 
+        def store(piece, tt, lo, hi):
+            nc.sync.dma_start(
+                out=out_rows[tt * P : (tt + 1) * P, piece * PIECE + lo : piece * PIECE + hi],
+                in_=results[tt][:, lo:hi],
+            )
+
         def multiply_and_store(piece, columns_per_store):
-            for tt in range(TOKEN_TILES):
-                for b in range(BANKS_PER_PIECE):
+            for b in range(BANKS_PER_PIECE):
+                for tt in range(TOKEN_TILES):
                     cols = slice(b * BANK, (b + 1) * BANK)
                     nc.vector.tensor_tensor(
                         out=results[tt][:, cols], in0=results[tt][:, cols],
@@ -330,18 +338,12 @@ def tile_neuronllamamlp_pa_kernel(
                     )
                     done = (b + 1) * BANK
                     if done % columns_per_store == 0:
-                        nc.sync.dma_start(
-                            out=out_rows[
-                                tt * P : (tt + 1) * P,
-                                piece * PIECE + done - columns_per_store : piece * PIECE + done,
-                            ],
-                            in_=results[tt][:, done - columns_per_store : done],
-                        )
+                        store(piece, tt, done - columns_per_store, done)
 
         on_vector = nc.vector.tensor_copy
         on_scalar = nc.scalar.copy
 
-        gain_rows = const.tile([P, BANK], BF16)
+        gain_rows = const.tile([P, P], BF16)
         nc.vector.memset(gain_rows[:], 0.0)
         eps = const.tile([P, 1], F32)
         nc.vector.memset(eps[:], EPS)
@@ -353,37 +355,42 @@ def tile_neuronllamamlp_pa_kernel(
         make_identity(nc, ident[:])
 
         load_v(GATE, 0)
-        load_v(GATE, 1)
         nc.sync.dma_start(
-            out=gain_rows[0:H_PASSES, :], in_=ln_w.rearrange("(g c) -> g c", c=BANK)
+            out=gain_rows[0:GAIN_ROWS, :], in_=ln_w.rearrange("(g c) -> g c", c=P)
         )
         load_tokens(0)
+        load_v(GATE, 1)
         load_v(GATE, 2)
         load_v(GATE, 3)
         load_tokens(1)
         for g in range(H_PASSES):
             load_v(UP, g)
-        for piece in range(LOADS_AHEAD):
+        for piece in range(U_PIECES):
             load_u(piece)
-        regroup_v(on_vector, GATE, 0)
-        regroup_v(on_vector, GATE, 1, 0, 2)
-        regroup_v(on_scalar, GATE, 1, 2, PACK)
-        spread_gain()
+        regroup_v(on_vector, GATE, 0, 0, 2)
+        regroup_v(on_scalar, GATE, 0, 2, PACK)
+        turn_gain(on_vector)
+        quantise(("v", GATE, 0), 0, R)
+        spread_gain(on_vector, 0)
+        spread_gain(on_vector, 1)
         add_tokens(0)
         square_tokens(0)
         root_mean_square(0)
-        quantise_piece(("v", GATE, 0))
-        regroup_v(on_vector, GATE, 2)
-        regroup_v(on_vector, GATE, 3, 0, 2)
+        regroup_v(on_vector, GATE, 1)
+        quantise(("v", GATE, 0), R, PIECE)
+        regroup_v(on_vector, GATE, 2, 0, 2)
+        regroup_v(on_scalar, GATE, 2, 2, PACK)
+        regroup_v(on_scalar, GATE, 3, 2, PACK)
         add_tokens(1)
         square_tokens(1)
         root_mean_square(1)
         normalise(0)
         gpsimd_waits_for_rstd(0)
-        regroup_v_on_gpsimd(GATE, 3, 2, PACK)
+        regroup_v_on_gpsimd(GATE, 3, 0, 2)
         transpose_tokens(0)
-        quantise_piece(("v", GATE, 1))
+        quantise(("v", GATE, 1), 0, PIECE)
         regroup_v(on_vector, UP, 0)
+        regroup_v(on_vector, UP, 1, 0, 2)
         nc.scalar.activation(out=warm[:, 1:2], in_=eps[:], func=ACT.Silu)
         regroup_tokens(on_scalar, 0)
         normalise(1)
@@ -392,50 +399,60 @@ def tile_neuronllamamlp_pa_kernel(
         transpose_tokens(1)
         quantise_tokens(0)
         first_product(GATE, 0)
-        regroup_v(on_scalar, UP, 1)
+        regroup_v(on_scalar, UP, 1, 2, PACK)
         regroup_tokens(on_scalar, 1)
         regroup_v(on_vector, UP, 2, 3, PACK)
-        regroup_v(on_vector, UP, 3)
-        quantise_piece(("v", UP, 0))
+        regroup_v(on_vector, UP, 3, 0, 2)
+        regroup_v(on_scalar, UP, 3, 2, PACK)
+        quantise(("v", UP, 0), 0, PIECE)
         quantise_tokens(1)
         first_product(GATE, 1)
-        two_grouped_parts(("u", UP, 0))
+        first_grouped_part(("u", UP, 0))
         regroup(on_scalar, ("u", UP, 0), 0, HALF)
-        quantise_piece(("v", UP, 1))
+        quantise(("v", UP, 1), 0, PIECE)
         first_product(UP, 0)
         first_product(UP, 1)
         one_grouped_part(("u", GATE, 0))
         regroup(on_vector, ("u", GATE, 0), 0, PIECE)
         round_first_product(on_scalar, GATE, 0)
         round_first_product(on_scalar, GATE, 1)
-        regroup(on_scalar, ("u", UP, 0), HALF, PIECE)
-        quantise_piece(("u", GATE, 0))
+        second_grouped_part(("u", UP, 0))
+        regroup(on_scalar, ("u", UP, 0), HALF + TENSOR_COLS, PIECE)
+        quantise(("u", GATE, 0), 0, PIECE)
         round_first_product(on_scalar, UP, 0)
         round_first_product(on_scalar, UP, 1)
+        regroup_through_psum(("u", UP, 0), HALF, HALF + TENSOR_COLS)
         one_grouped_part(("u", GATE, 1))
         regroup(on_vector, ("u", GATE, 1), 0, HALF)
-        quantise_piece(("u", UP, 0))
+        quantise(("u", UP, 0), 0, HALF)
         quantise_first_products()
         regroup(on_vector, ("u", GATE, 1), HALF, PIECE)
-        two_grouped_parts(("u", UP, 1))
-        regroup(on_scalar, ("u", UP, 1), 0, HALF)
-        regroup(on_vector, ("u", UP, 1), HALF, PIECE)
+        first_grouped_part(("u", UP, 1))
+        regroup_through_psum(("u", UP, 1), 0, TENSOR_COLS)
+        regroup(on_scalar, ("u", UP, 1), TENSOR_COLS, HALF)
 
         for s in range(U_PIECES):
-            load_u(s + LOADS_AHEAD)
-            second_products(s)
+            for tt in range(TOKEN_TILES):
+                for b in range(BANKS_PER_PIECE):
+                    second_product(GATE, s, tt, b)
             silu_of_gate()
             if s + 2 < U_PIECES:
                 one_grouped_part(("u", GATE, s + 2))
                 regroup(on_vector, ("u", GATE, s + 2), 0, GATE_VECTOR_COLS)
                 regroup(on_scalar, ("u", GATE, s + 2), GATE_VECTOR_COLS, PIECE)
             if s + 1 < U_PIECES:
-                quantise_piece(("u", GATE, s + 1))
-                quantise_piece(("u", UP, s + 1))
+                quantise(("u", GATE, s + 1), 0, PIECE)
+                quantise(("u", UP, s + 1), 0, HALF)
             if s + 2 < U_PIECES:
-                two_grouped_parts(("u", UP, s + 2))
+                first_grouped_part(("u", UP, s + 2))
                 regroup_through_psum(("u", UP, s + 2), 0, TENSOR_COLS)
                 regroup(on_scalar, ("u", UP, s + 2), TENSOR_COLS, HALF)
-                regroup(on_scalar, ("u", UP, s + 2), HALF, GPSIMD_FROM)
-                regroup_on_gpsimd(("u", UP, s + 2), GPSIMD_FROM, PIECE)
-            multiply_and_store(s, PIECE if s + 1 < U_PIECES else BANK)
+            quantise(("u", UP, s), HALF, PIECE)
+            for b in range(BANKS_PER_PIECE):
+                for tt in range(TOKEN_TILES):
+                    second_product(UP, s, tt, b)
+            if s + 1 < U_PIECES:
+                second_grouped_part(("u", UP, s + 1))
+                regroup(on_scalar, ("u", UP, s + 1), HALF, GPSIMD_FROM)
+                regroup_on_gpsimd(("u", UP, s + 1), GPSIMD_FROM, PIECE)
+            multiply_and_store(s, PIECE if s + 2 < U_PIECES else BANK)

@@ -31,15 +31,14 @@ U_PIECES = I // PIECE
 RUN = 4
 GATE = 0
 UP = 1
-GATE_VECTOR_COLS = 640
+GATE_VECTOR_COLS = 656
 TENSOR_COLS = 224
 GPSIMD_FROM = 640
-RAW_SLOTS = 12
+RAW_SLOTS = 15
 GROUPED_SLOTS = 4
 UP_FIRST_HALF_SLOTS = 2
 UP_SECOND_HALF_SLOTS = 1
 CODE_SLOTS = 7
-RESULT_SLOTS = 8
 PSUM_BANKS = 8
 
 FLOPS = 2 * TOKENS * (2 * H * R + 2 * R * I)
@@ -64,14 +63,12 @@ def tile_neuronllamamlp_pa_kernel(
         up_first_pool = ctx.enter_context(tc.tile_pool(name="up_a", bufs=UP_FIRST_HALF_SLOTS))
         up_second_pool = ctx.enter_context(tc.tile_pool(name="up_b", bufs=UP_SECOND_HALF_SLOTS))
         code_pool = ctx.enter_context(tc.tile_pool(name="codes", bufs=CODE_SLOTS))
-        result_pool = ctx.enter_context(tc.tile_pool(name="result", bufs=RESULT_SLOTS))
         psum = ctx.enter_context(tc.psum_pool(name="psum", bufs=PSUM_BANKS))
         ctx.enter_context(tc.manual_schedule())
 
         gain = keep.tile([P, H], BF16)
         gain_cols = keep.tile([P, GAIN_ROWS], BF16)
         junk = keep.tile([P, BANK], BF16)
-        gp_junk = keep.tile([P, 1], F32)
         n_grouped = keep.tile([P, TOKEN_TILES, H_PASSES * P, PACK], BF16, align_bytes=64)
         n_codes = keep.tile([P, TOKEN_TILES, H_PASSES, P], U32, align_bytes=64)
         n_scales = keep.tile([P, TOKEN_TILES, H_PASSES, P], U8, align_bytes=64)
@@ -79,7 +76,7 @@ def tile_neuronllamamlp_pa_kernel(
         r_codes = keep.tile([P, 2, TOKEN_TILES, P], U32, align_bytes=64)
         r_scales = keep.tile([P, 2, TOKEN_TILES, P], U8, align_bytes=64)
 
-        x_res, h, n, sum_sq, rms, rstd, n_t = {}, {}, {}, {}, {}, {}, {}
+        x_res, h, n, sum_sq, rstd, n_t = {}, {}, {}, {}, {}, {}
         raw, grouped_parts, codes, scales = {}, {}, {}, {}
         r_t, banks, results = {}, {}, {}
 
@@ -123,22 +120,20 @@ def tile_neuronllamamlp_pa_kernel(
                     accum_out=sum_sq[tt][:, g : g + 1],
                 )
 
-        def root_mean_square(tt):
+        def reciprocal_rms(tt):
             scaled = small.tile([P, H_PASSES], F32, name="scaled")
             mean_sq = small.tile([P, 1], F32, name="mean_sq")
             nc.scalar.activation(
                 out=scaled[:], in_=sum_sq[tt][:], func=ACT.Copy, scale=1.0 / H,
-                accum_out=mean_sq[:, 0:1],
+                bias=EPS / H_PASSES, accum_out=mean_sq[:, 0:1],
             )
-            rms[tt] = small.tile([P, 1], F32, name="rms")
-            nc.scalar.activation(
-                out=rms[tt][:], in_=mean_sq[:, 0:1], func=ACT.Sqrt, bias=eps[:, 0:1]
+            rstd[tt] = small.tile([P, 1], F32, name="rstd")
+            nc.gpsimd.tensor_tensor(
+                out=rstd[tt][:], in0=mean_sq[:], in1=minus_half[:], op=ALU.pow
             )
 
         def normalise(tt):
-            rstd[tt] = small.tile([P, 1], F32, name="rstd")
-            nc.vector.reciprocal(rstd[tt][:], rms[tt][:])
-            n[tt] = result_pool.tile([P, H], BF16, tag="result", name="n")
+            n[tt] = small.tile([P, H], BF16, name="n")
             for g in range(H_PASSES):
                 cols = slice(g * BANK, (g + 1) * BANK)
                 nc.vector.scalar_tensor_tensor(
@@ -239,27 +234,36 @@ def tile_neuronllamamlp_pa_kernel(
                 scalar1=1.0, scalar2=0.0, op0=ALU.mult, op1=ALU.add,
             )
 
-        def regroup_through_psum(key, lo, hi):
-            bank = psum.tile([P, hi - lo, PACK], BF16, tag="bank", name="grouped_bank")
-            middle = (lo + hi) // 2
-            for c0, c1 in ((lo, middle), (middle, hi)):
+        def copy_through_psum(grouped, columns):
+            count = grouped.shape[1]
+            bank = psum.tile([P, count, PACK], BF16, tag="bank", name="grouped_bank")
+            for half in range(2):
+                part = slice(half * count // 2, (half + 1) * count // 2)
                 nc.tensor.matmul(
-                    bank[:, c0 - lo : c1 - lo, :], lhsT=ident_bf[:],
-                    rhs=raw[key][:, :, c0:c1].rearrange("p j c -> p c j"),
-                    start=True, stop=True,
+                    bank[:, part, :], lhsT=ident_bf[:], rhs=columns[half], start=True, stop=True
                 )
-            nc.scalar.copy(out=grouped_columns(key, lo, hi), in_=bank[:])
+            nc.scalar.copy(out=grouped, in_=bank[:])
+
+        def regroup_through_psum(key, lo, hi):
+            middle = (lo + hi) // 2
+            copy_through_psum(
+                grouped_columns(key, lo, hi),
+                [raw[key][:, :, a:b].rearrange("p j c -> p c j") for a, b in ((lo, middle), (middle, hi))],
+            )
+
+        def regroup_v_through_psum(m, g, t0):
+            start = (g % 2) * R + P * t0
+            grouped, rows = first_factor_views(m, g, t0, t0 + 2)
+            copy_through_psum(
+                grouped_columns(("v", m, g // 2), start, start + 2 * P),
+                [rows[:, :, :, t].rearrange("p j m -> p m j") for t in range(2)],
+            )
 
         def regroup_on_gpsimd(key, lo, hi):
             nc.gpsimd.tensor_scalar(
                 out=grouped_columns(key, lo, hi),
                 in0=raw[key][:, :, lo:hi].rearrange("p j c -> p c j"),
                 scalar1=1.0, scalar2=0.0, op0=ALU.mult, op1=ALU.add,
-            )
-
-        def gpsimd_waits_for_rstd(tt):
-            nc.gpsimd.tensor_scalar(
-                out=gp_junk[:], in0=rstd[tt][:], scalar1=1.0, scalar2=0.0, op0=ALU.mult, op1=ALU.add,
             )
 
         def quantise(key, lo, hi):
@@ -300,23 +304,27 @@ def tile_neuronllamamlp_pa_kernel(
                 in_=r_grouped[:].rearrange("p m a t j -> p (m a t j)"),
             )
 
-        def second_product(m, piece, tt, b):
-            cols = slice(b * BANK, (b + 1) * BANK)
-            banks[m, tt, b] = psum.tile([P, BANK], F32, tag="bank", name="bank")
-            nc.tensor.matmul_mx(
-                out=banks[m, tt, b][:],
-                lhsT=r_codes[:, m, tt, :].bitcast(FP8X4),
-                lhsT_scale=r_scales[:, m, tt, :],
-                rhs=codes["u", m, piece][:, cols].bitcast(FP8X4),
-                rhs_scale=scales["u", m, piece][:, cols],
-                start=True,
-                stop=True,
-            )
+        def second_products(m, piece, halves):
+            for b in halves:
+                cols = slice(b * BANK, (b + 1) * BANK)
+                for tt in range(TOKEN_TILES):
+                    banks[m, tt, b] = psum.tile([P, BANK], F32, tag="bank", name="bank")
+                    nc.tensor.matmul_mx(
+                        out=banks[m, tt, b][:],
+                        lhsT=r_codes[:, m, tt, :].bitcast(FP8X4),
+                        lhsT_scale=r_scales[:, m, tt, :],
+                        rhs=codes["u", m, piece][:, cols].bitcast(FP8X4),
+                        rhs_scale=scales["u", m, piece][:, cols],
+                        start=True,
+                        stop=True,
+                    )
 
         def silu_of_gate():
+            both = raw_pool.tile([P, TOKEN_TILES, PIECE], F32, tag="raw", name="results")
             for tt in range(TOKEN_TILES):
-                results[tt] = result_pool.tile([P, PIECE], F32, tag="result", name="result")
-                for b in range(BANKS_PER_PIECE):
+                results[tt] = both[:, tt, :]
+            for b in range(BANKS_PER_PIECE):
+                for tt in range(TOKEN_TILES):
                     nc.scalar.activation(
                         out=results[tt][:, b * BANK : (b + 1) * BANK],
                         in_=banks[GATE, tt, b][:], func=ACT.Silu,
@@ -345,10 +353,10 @@ def tile_neuronllamamlp_pa_kernel(
 
         gain_rows = const.tile([P, P], BF16)
         nc.vector.memset(gain_rows[:], 0.0)
-        eps = const.tile([P, 1], F32)
-        nc.vector.memset(eps[:], EPS)
-        warm = const.tile([P, 2], F32)
-        nc.scalar.sqrt(warm[:, 0:1], eps[:])
+        minus_half = const.tile([P, 1], F32)
+        nc.vector.memset(minus_half[:], -0.5)
+        warm = const.tile([P, 1], F32)
+        nc.scalar.activation(out=warm[:], in_=minus_half[:], func=ACT.Silu)
         ident_bf = const.tile([P, P], BF16)
         make_identity(nc, ident_bf[:])
         ident = const.tile([P, P], F32)
@@ -372,34 +380,31 @@ def tile_neuronllamamlp_pa_kernel(
         turn_gain(on_vector)
         quantise(("v", GATE, 0), 0, R)
         spread_gain(on_vector, 0)
-        spread_gain(on_vector, 1)
         add_tokens(0)
         square_tokens(0)
-        root_mean_square(0)
+        reciprocal_rms(0)
         regroup_v(on_vector, GATE, 1)
-        quantise(("v", GATE, 0), R, PIECE)
         regroup_v(on_vector, GATE, 2, 0, 2)
+        quantise(("v", GATE, 0), R, PIECE)
+        spread_gain(on_vector, 1)
         regroup_v(on_scalar, GATE, 2, 2, PACK)
         regroup_v(on_scalar, GATE, 3, 2, PACK)
+        regroup_v_on_gpsimd(GATE, 3, 0, 2)
         add_tokens(1)
         square_tokens(1)
-        root_mean_square(1)
+        reciprocal_rms(1)
         normalise(0)
-        gpsimd_waits_for_rstd(0)
-        regroup_v_on_gpsimd(GATE, 3, 0, 2)
         transpose_tokens(0)
         quantise(("v", GATE, 1), 0, PIECE)
         regroup_v(on_vector, UP, 0)
-        regroup_v(on_vector, UP, 1, 0, 2)
-        nc.scalar.activation(out=warm[:, 1:2], in_=eps[:], func=ACT.Silu)
+        regroup_v(on_vector, UP, 1, 0, 1)
         regroup_tokens(on_scalar, 0)
         normalise(1)
-        gpsimd_waits_for_rstd(1)
         regroup_v_on_gpsimd(UP, 2, 0, 3)
         transpose_tokens(1)
         quantise_tokens(0)
         first_product(GATE, 0)
-        regroup_v(on_scalar, UP, 1, 2, PACK)
+        regroup_v(on_scalar, UP, 1, 1, PACK)
         regroup_tokens(on_scalar, 1)
         regroup_v(on_vector, UP, 2, 3, PACK)
         regroup_v(on_vector, UP, 3, 0, 2)
@@ -418,23 +423,21 @@ def tile_neuronllamamlp_pa_kernel(
         round_first_product(on_scalar, GATE, 1)
         second_grouped_part(("u", UP, 0))
         regroup(on_scalar, ("u", UP, 0), HALF + TENSOR_COLS, PIECE)
+        one_grouped_part(("u", GATE, 1))
+        regroup(on_vector, ("u", GATE, 1), 0, HALF)
         quantise(("u", GATE, 0), 0, PIECE)
         round_first_product(on_scalar, UP, 0)
         round_first_product(on_scalar, UP, 1)
         regroup_through_psum(("u", UP, 0), HALF, HALF + TENSOR_COLS)
-        one_grouped_part(("u", GATE, 1))
-        regroup(on_vector, ("u", GATE, 1), 0, HALF)
-        quantise(("u", UP, 0), 0, HALF)
         quantise_first_products()
+        quantise(("u", UP, 0), 0, HALF)
         regroup(on_vector, ("u", GATE, 1), HALF, PIECE)
         first_grouped_part(("u", UP, 1))
         regroup_through_psum(("u", UP, 1), 0, TENSOR_COLS)
         regroup(on_scalar, ("u", UP, 1), TENSOR_COLS, HALF)
 
         for s in range(U_PIECES):
-            for tt in range(TOKEN_TILES):
-                for b in range(BANKS_PER_PIECE):
-                    second_product(GATE, s, tt, b)
+            second_products(GATE, s, range(BANKS_PER_PIECE))
             silu_of_gate()
             if s + 2 < U_PIECES:
                 one_grouped_part(("u", GATE, s + 2))
@@ -442,15 +445,15 @@ def tile_neuronllamamlp_pa_kernel(
                 regroup(on_scalar, ("u", GATE, s + 2), GATE_VECTOR_COLS, PIECE)
             if s + 1 < U_PIECES:
                 quantise(("u", GATE, s + 1), 0, PIECE)
-                quantise(("u", UP, s + 1), 0, HALF)
             if s + 2 < U_PIECES:
                 first_grouped_part(("u", UP, s + 2))
                 regroup_through_psum(("u", UP, s + 2), 0, TENSOR_COLS)
                 regroup(on_scalar, ("u", UP, s + 2), TENSOR_COLS, HALF)
+            second_products(UP, s, [0])
             quantise(("u", UP, s), HALF, PIECE)
-            for b in range(BANKS_PER_PIECE):
-                for tt in range(TOKEN_TILES):
-                    second_product(UP, s, tt, b)
+            second_products(UP, s, [1])
+            if s + 1 < U_PIECES:
+                quantise(("u", UP, s + 1), 0, HALF)
             if s + 1 < U_PIECES:
                 second_grouped_part(("u", UP, s + 1))
                 regroup(on_scalar, ("u", UP, s + 1), HALF, GPSIMD_FROM)

from contextlib import ExitStack

import concourse.mybir as mybir
from concourse.masks import make_identity

F32 = mybir.dt.float32
BF16 = mybir.dt.bfloat16
U32 = mybir.dt.uint32
U8 = mybir.dt.uint8
FP8X4 = mybir.dt.float8_e4m3fn_x4
ACT = mybir.ActivationFunctionType
ALU = mybir.AluOpType

P = 128
PACK = 4
K_PASS = P * PACK
TOKENS = 256
TOKEN_TILES = TOKENS // P
H = 2048
H_PASSES = H // K_PASS
GAIN_ROWS = H // P
R = 512
I = 7168
EPS = 1e-05
BANK = 512
HALF = 512
PIECE = 2 * HALF
BANKS_PER_PIECE = PIECE // BANK
V_PIECES = H_PASSES * R // PIECE
U_PIECES = I // PIECE
RUN = 4
GATE = 0
UP = 1
GATE_VECTOR_COLS = 656
TENSOR_COLS = 224
GPSIMD_FROM = 640
RAW_SLOTS = 15
GROUPED_SLOTS = 4
UP_FIRST_HALF_SLOTS = 2
UP_SECOND_HALF_SLOTS = 1
CODE_SLOTS = 7
PSUM_BANKS = 8

FLOPS = 2 * TOKENS * (2 * H * R + 2 * R * I)


def tile_neuronllamamlp_pa_kernel(
    tc, x, residual, ln_w, w_gate_v, w_gate_u, w_up_v, w_up_u, out
):
    nc = tc.nc
    x_rows = x.flatten_outer_dims()
    res_rows = residual.flatten_outer_dims()
    out_rows = out.flatten_outer_dims()
    v_views = [w.rearrange("(g p j) r -> p g j r", j=PACK, p=P) for w in (w_gate_v, w_up_v)]
    u_views = [w.rearrange("(p j) i -> p j i", j=PACK) for w in (w_gate_u, w_up_u)]

    with ExitStack() as ctx:
        const = ctx.enter_context(tc.tile_pool(name="const", bufs=1))
        keep = ctx.enter_context(tc.tile_pool(name="keep", bufs=1))
        small = ctx.enter_context(tc.tile_pool(name="small", bufs=TOKEN_TILES))
        raw_pool = ctx.enter_context(tc.tile_pool(name="raw", bufs=RAW_SLOTS))
        grouped_pool = ctx.enter_context(tc.tile_pool(name="grouped", bufs=GROUPED_SLOTS))
        up_first_pool = ctx.enter_context(tc.tile_pool(name="up_a", bufs=UP_FIRST_HALF_SLOTS))
        up_second_pool = ctx.enter_context(tc.tile_pool(name="up_b", bufs=UP_SECOND_HALF_SLOTS))
        code_pool = ctx.enter_context(tc.tile_pool(name="codes", bufs=CODE_SLOTS))
        psum = ctx.enter_context(tc.psum_pool(name="psum", bufs=PSUM_BANKS))
        ctx.enter_context(tc.manual_schedule())

        gain = keep.tile([P, H], BF16)
        gain_cols = keep.tile([P, GAIN_ROWS], BF16)
        junk = keep.tile([P, BANK], BF16)
        n_grouped = keep.tile([P, TOKEN_TILES, H_PASSES * P, PACK], BF16, align_bytes=64)
        n_codes = keep.tile([P, TOKEN_TILES, H_PASSES, P], U32, align_bytes=64)
        n_scales = keep.tile([P, TOKEN_TILES, H_PASSES, P], U8, align_bytes=64)
        r_grouped = keep.tile([P, 2, TOKEN_TILES, P, PACK], BF16, align_bytes=64)
        r_codes = keep.tile([P, 2, TOKEN_TILES, P], U32, align_bytes=64)
        r_scales = keep.tile([P, 2, TOKEN_TILES, P], U8, align_bytes=64)

        x_res, h, n, sum_sq, rstd, n_t = {}, {}, {}, {}, {}, {}
        raw, grouped_parts, codes, scales = {}, {}, {}, {}
        r_t, banks, results = {}, {}, {}

        def load_tokens(tt):
            rows = slice(tt * P, (tt + 1) * P)
            x_res[tt] = raw_pool.tile([P, 2, H], BF16, tag="raw", name="x_res")
            nc.sync.dma_start(out=x_res[tt][:, 0, :], in_=x_rows[rows, :])
            nc.sync.dma_start(out=x_res[tt][:, 1, :], in_=res_rows[rows, :])

        def turn_gain(copy):
            columns = psum.tile([P, P], BF16, tag="bank", name="gain_columns")
            nc.tensor.transpose(columns[:], gain_rows[:], ident_bf[:])
            copy(out=gain_cols[:], in_=columns[:, 0:GAIN_ROWS])

        def spread_gain(copy, half):
            bank = psum.tile([P, 2 * BANK], BF16, tag="bank", name="gain_bank")
            for i in range(GAIN_ROWS // 2):
                g = half * (GAIN_ROWS // 2) + i
                nc.tensor.transpose(
                    bank[:, i * P : (i + 1) * P],
                    gain_cols[:, g : g + 1].to_broadcast([P, P]),
                    ident_bf[:],
                )
            copy(out=gain[:, half * 2 * BANK : (half + 1) * 2 * BANK], in_=bank[:])

        def add_tokens(tt):
            for g in range(H_PASSES):
                cols = slice(g * BANK, (g + 1) * BANK)
                h[tt, g] = psum.tile([P, BANK], F32, tag="bank", name="h")
                for part in range(2):
                    nc.tensor.matmul(
                        h[tt, g][:], lhsT=ident_bf[:], rhs=x_res[tt][:, part, cols],
                        start=(part == 0), stop=(part == 1),
                    )

        def square_tokens(tt):
            sum_sq[tt] = small.tile([P, H_PASSES], F32, name="sum_sq")
            for g in range(H_PASSES):
                nc.scalar.activation(
                    out=junk[:], in_=h[tt, g][:], func=ACT.Square,
                    accum_out=sum_sq[tt][:, g : g + 1],
                )

        def reciprocal_rms(tt):
            scaled = small.tile([P, H_PASSES], F32, name="scaled")
            mean_sq = small.tile([P, 1], F32, name="mean_sq")
            nc.scalar.activation(
                out=scaled[:], in_=sum_sq[tt][:], func=ACT.Copy, scale=1.0 / H,
                bias=EPS / H_PASSES, accum_out=mean_sq[:, 0:1],
            )
            rstd[tt] = small.tile([P, 1], F32, name="rstd")
            nc.gpsimd.tensor_tensor(
                out=rstd[tt][:], in0=mean_sq[:], in1=minus_half[:], op=ALU.pow
            )

        def normalise(tt):
            n[tt] = small.tile([P, H], BF16, name="n")
            for g in range(H_PASSES):
                cols = slice(g * BANK, (g + 1) * BANK)
                nc.vector.scalar_tensor_tensor(
                    out=n[tt][:, cols], in0=h[tt, g][:], scalar=rstd[tt][:, 0:1],
                    in1=gain[:, cols], op0=ALU.mult, op1=ALU.mult,
                )

        def transpose_tokens(tt):
            words = n[tt][:].bitcast(F32)
            for half in range(2):
                n_t[tt, half] = psum.tile([P, 2, 2, P], F32, tag="bank", name="n_t")
                for b in range(2):
                    g = 2 * half + b
                    for u in range(2):
                        nc.tensor.transpose(
                            n_t[tt, half][:, b, u, :],
                            words[:, 2 * P * g + u : 2 * P * (g + 1) : 2],
                            ident[:],
                        )

        def regroup_tokens(copy, tt):
            words = n_grouped[:, tt].rearrange("p c j -> p (c j)").bitcast(F32)
            words = words.rearrange("p (g t u) -> p g t u", g=H_PASSES, u=2)
            for half in range(2):
                copy(
                    out=words[:, 2 * half : 2 * half + 2],
                    in_=n_t[tt, half][:].rearrange("p g u t -> p g t u"),
                )

        def quantise_tokens(tt):
            nc.vector.quantize_mx(
                out=n_codes[:, tt].rearrange("p g t -> p (g t)").bitcast(FP8X4),
                scales=n_scales[:, tt].rearrange("p g t -> p (g t)"),
                in_=n_grouped[:, tt].rearrange("p c j -> p (c j)"),
            )

        def load_v(m, g):
            key = ("v", m, g // 2)
            if g % 2 == 0:
                raw[key] = raw_pool.tile([P, 2, PACK, R], BF16, tag="raw", name="raw_v")
            nc.sync.dma_start(out=raw[key][:, g % 2, :, :], in_=v_views[m][:, g, :, :])

        def load_u(piece):
            for m in (GATE, UP):
                key = ("u", m, piece)
                raw[key] = raw_pool.tile([P, PACK, PIECE], BF16, tag="raw", name="raw_u")
                nc.sync.dma_start(
                    out=raw[key][:], in_=u_views[m][:, :, piece * PIECE : (piece + 1) * PIECE]
                )

        def one_grouped_part(key):
            whole = grouped_pool.tile([P, PIECE, PACK], BF16, align_bytes=64, name="grouped")
            grouped_parts[key] = [(0, PIECE, whole)]

        def first_grouped_part(key):
            first = up_first_pool.tile([P, HALF, PACK], BF16, align_bytes=64, name="up_first")
            grouped_parts[key] = [(0, HALF, first)]

        def second_grouped_part(key):
            second = up_second_pool.tile([P, HALF, PACK], BF16, align_bytes=64, name="up_second")
            grouped_parts[key].append((HALF, PIECE, second))

        def grouped_columns(key, lo, hi):
            views = [
                part[:, lo - start : hi - start, :]
                for start, end, part in grouped_parts[key]
                if start <= lo and hi <= end
            ]
            return views[0]

        def regroup(copy, key, lo, hi):
            copy(
                out=grouped_columns(key, lo, hi).rearrange("p (c i) j -> p c j i", i=RUN),
                in_=raw[key][:, :, lo:hi].rearrange("p j (c i) -> p c j i", i=RUN),
            )

        def first_factor_views(m, g, t0, t1):
            key = ("v", m, g // 2)
            if key not in grouped_parts:
                one_grouped_part(key)
            start = (g % 2) * R
            grouped = grouped_columns(key, start + P * t0, start + P * t1)
            rows = raw[key][:, g % 2, :, :].rearrange("p j (m t) -> p j m t", t=PACK)
            return grouped.rearrange("p (t m) j -> p t m j", m=P), rows[:, :, :, t0:t1]

        def regroup_v(copy, m, g, t0=0, t1=PACK):
            grouped, rows = first_factor_views(m, g, t0, t1)
            copy(
                out=grouped.rearrange("p t (m i) j -> p t m j i", i=2),
                in_=rows.rearrange("p j (m i) t -> p t m j i", i=2),
            )

        def regroup_v_on_gpsimd(m, g, t0, t1):
            grouped, rows = first_factor_views(m, g, t0, t1)
            nc.gpsimd.tensor_scalar(
                out=grouped,
                in0=rows.rearrange("p j m t -> p t m j"),
                scalar1=1.0, scalar2=0.0, op0=ALU.mult, op1=ALU.add,
            )

        def copy_through_psum(grouped, columns):
            count = grouped.shape[1]
            bank = psum.tile([P, count, PACK], BF16, tag="bank", name="grouped_bank")
            for half in range(2):
                part = slice(half * count // 2, (half + 1) * count // 2)
                nc.tensor.matmul(
                    bank[:, part, :], lhsT=ident_bf[:], rhs=columns[half], start=True, stop=True
                )
            nc.scalar.copy(out=grouped, in_=bank[:])

        def regroup_through_psum(key, lo, hi):
            middle = (lo + hi) // 2
            copy_through_psum(
                grouped_columns(key, lo, hi),
                [raw[key][:, :, a:b].rearrange("p j c -> p c j") for a, b in ((lo, middle), (middle, hi))],
            )

        def regroup_v_through_psum(m, g, t0):
            start = (g % 2) * R + P * t0
            grouped, rows = first_factor_views(m, g, t0, t0 + 2)
            copy_through_psum(
                grouped_columns(("v", m, g // 2), start, start + 2 * P),
                [rows[:, :, :, t].rearrange("p j m -> p m j") for t in range(2)],
            )

        def regroup_on_gpsimd(key, lo, hi):
            nc.gpsimd.tensor_scalar(
                out=grouped_columns(key, lo, hi),
                in0=raw[key][:, :, lo:hi].rearrange("p j c -> p c j"),
                scalar1=1.0, scalar2=0.0, op0=ALU.mult, op1=ALU.add,
            )

        def quantise(key, lo, hi):
            if key not in codes:
                codes[key] = code_pool.tile([P, PIECE], U32, align_bytes=64, name="codes")
                scales[key] = code_pool.tile([P, PIECE], U8, align_bytes=64, name="scales")
            nc.vector.quantize_mx(
                out=codes[key][:, lo:hi].bitcast(FP8X4),
                scales=scales[key][:, lo:hi],
                in_=grouped_columns(key, lo, hi).rearrange("p c j -> p (c j)"),
            )

        def first_product(m, tt):
            r_t[m, tt] = psum.tile([P, PACK, P], F32, tag="bank", name="r_t")
            for j in range(PACK):
                for g in range(H_PASSES):
                    key = ("v", m, g // 2)
                    r_cols = slice(R * (g % 2) + P * j, R * (g % 2) + P * (j + 1))
                    nc.tensor.matmul_mx(
                        out=r_t[m, tt][:, j, :],
                        lhsT=codes[key][:, r_cols].bitcast(FP8X4),
                        lhsT_scale=scales[key][:, r_cols],
                        rhs=n_codes[:, tt, g, :].bitcast(FP8X4),
                        rhs_scale=n_scales[:, tt, g, :],
                        start=(g == 0),
                        stop=(g == H_PASSES - 1),
                    )

        def round_first_product(copy, m, tt):
            copy(
                out=r_grouped[:, m, tt, :, :], in_=r_t[m, tt][:].rearrange("p j t -> p t j")
            )

        def quantise_first_products():
            nc.vector.quantize_mx(
                out=r_codes[:].rearrange("p m a t -> p (m a t)").bitcast(FP8X4),
                scales=r_scales[:].rearrange("p m a t -> p (m a t)"),
                in_=r_grouped[:].rearrange("p m a t j -> p (m a t j)"),
            )

        def second_products(m, piece, halves):
            for b in halves:
                cols = slice(b * BANK, (b + 1) * BANK)
                for tt in range(TOKEN_TILES):
                    banks[m, tt, b] = psum.tile([P, BANK], F32, tag="bank", name="bank")
                    nc.tensor.matmul_mx(
                        out=banks[m, tt, b][:],
                        lhsT=r_codes[:, m, tt, :].bitcast(FP8X4),
                        lhsT_scale=r_scales[:, m, tt, :],
                        rhs=codes["u", m, piece][:, cols].bitcast(FP8X4),
                        rhs_scale=scales["u", m, piece][:, cols],
                        start=True,
                        stop=True,
                    )

        def silu_of_gate():
            both = raw_pool.tile([P, TOKEN_TILES, PIECE], F32, tag="raw", name="results")
            for tt in range(TOKEN_TILES):
                results[tt] = both[:, tt, :]
            for b in range(BANKS_PER_PIECE):
                for tt in range(TOKEN_TILES):
                    nc.scalar.activation(
                        out=results[tt][:, b * BANK : (b + 1) * BANK],
                        in_=banks[GATE, tt, b][:], func=ACT.Silu,
                    )

        def store(piece, tt, lo, hi):
            nc.sync.dma_start(
                out=out_rows[tt * P : (tt + 1) * P, piece * PIECE + lo : piece * PIECE + hi],
                in_=results[tt][:, lo:hi],
            )

        def multiply_and_store(piece, columns_per_store):
            for b in range(BANKS_PER_PIECE):
                for tt in range(TOKEN_TILES):
                    cols = slice(b * BANK, (b + 1) * BANK)
                    nc.vector.tensor_tensor(
                        out=results[tt][:, cols], in0=results[tt][:, cols],
                        in1=banks[UP, tt, b][:], op=ALU.mult,
                    )
                    done = (b + 1) * BANK
                    if done % columns_per_store == 0:
                        store(piece, tt, done - columns_per_store, done)

        on_vector = nc.vector.tensor_copy
        on_scalar = nc.scalar.copy

        gain_rows = const.tile([P, P], BF16)
        nc.vector.memset(gain_rows[:], 0.0)
        minus_half = const.tile([P, 1], F32)
        nc.vector.memset(minus_half[:], -0.5)
        warm = const.tile([P, 1], F32)
        nc.scalar.activation(out=warm[:], in_=minus_half[:], func=ACT.Silu)
        ident_bf = const.tile([P, P], BF16)
        make_identity(nc, ident_bf[:])
        ident = const.tile([P, P], F32)
        make_identity(nc, ident[:])

        load_v(GATE, 0)
        nc.sync.dma_start(
            out=gain_rows[0:GAIN_ROWS, :], in_=ln_w.rearrange("(g c) -> g c", c=P)
        )
        load_tokens(0)
        load_v(GATE, 1)
        load_v(GATE, 2)
        load_v(GATE, 3)
        load_tokens(1)
        for g in range(H_PASSES):
            load_v(UP, g)
        for piece in range(U_PIECES):
            load_u(piece)
        regroup_v(on_vector, GATE, 0, 0, 2)
        regroup_v(on_scalar, GATE, 0, 2, PACK)
        turn_gain(on_vector)
        quantise(("v", GATE, 0), 0, R)
        spread_gain(on_vector, 0)
        add_tokens(0)
        square_tokens(0)
        reciprocal_rms(0)
        regroup_v(on_vector, GATE, 1)
        regroup_v(on_vector, GATE, 2, 0, 2)
        quantise(("v", GATE, 0), R, PIECE)
        spread_gain(on_vector, 1)
        regroup_v(on_scalar, GATE, 2, 2, PACK)
        regroup_v(on_scalar, GATE, 3, 2, PACK)
        regroup_v_on_gpsimd(GATE, 3, 0, 2)
        add_tokens(1)
        square_tokens(1)
        reciprocal_rms(1)
        normalise(0)
        transpose_tokens(0)
        quantise(("v", GATE, 1), 0, PIECE)
        regroup_v(on_vector, UP, 0)
        regroup_v(on_vector, UP, 1, 0, 1)
        regroup_tokens(on_scalar, 0)
        normalise(1)
        regroup_v_on_gpsimd(UP, 2, 0, 3)
        transpose_tokens(1)
        quantise_tokens(0)
        first_product(GATE, 0)
        regroup_v(on_scalar, UP, 1, 1, PACK)
        regroup_tokens(on_scalar, 1)
        regroup_v(on_vector, UP, 2, 3, PACK)
        regroup_v(on_vector, UP, 3, 0, 2)
        regroup_v(on_scalar, UP, 3, 2, PACK)
        quantise(("v", UP, 0), 0, PIECE)
        quantise_tokens(1)
        first_product(GATE, 1)
        first_grouped_part(("u", UP, 0))
        regroup(on_scalar, ("u", UP, 0), 0, HALF)
        quantise(("v", UP, 1), 0, PIECE)
        first_product(UP, 0)
        first_product(UP, 1)
        one_grouped_part(("u", GATE, 0))
        regroup(on_vector, ("u", GATE, 0), 0, PIECE)
        round_first_product(on_scalar, GATE, 0)
        round_first_product(on_scalar, GATE, 1)
        second_grouped_part(("u", UP, 0))
        regroup(on_scalar, ("u", UP, 0), HALF + TENSOR_COLS, PIECE)
        one_grouped_part(("u", GATE, 1))
        regroup(on_vector, ("u", GATE, 1), 0, HALF)
        quantise(("u", GATE, 0), 0, PIECE)
        round_first_product(on_scalar, UP, 0)
        round_first_product(on_scalar, UP, 1)
        regroup_through_psum(("u", UP, 0), HALF, HALF + TENSOR_COLS)
        quantise_first_products()
        quantise(("u", UP, 0), 0, HALF)
        regroup(on_vector, ("u", GATE, 1), HALF, PIECE)
        first_grouped_part(("u", UP, 1))
        regroup_through_psum(("u", UP, 1), 0, TENSOR_COLS)
        regroup(on_scalar, ("u", UP, 1), TENSOR_COLS, HALF)

        for s in range(U_PIECES):
            second_products(GATE, s, range(BANKS_PER_PIECE))
            silu_of_gate()
            if s + 2 < U_PIECES:
                one_grouped_part(("u", GATE, s + 2))
                regroup(on_vector, ("u", GATE, s + 2), 0, GATE_VECTOR_COLS)
                regroup(on_scalar, ("u", GATE, s + 2), GATE_VECTOR_COLS, PIECE)
            if s + 1 < U_PIECES:
                quantise(("u", GATE, s + 1), 0, PIECE)
            if s + 2 < U_PIECES:
                first_grouped_part(("u", UP, s + 2))
                regroup_through_psum(("u", UP, s + 2), 0, TENSOR_COLS)
                regroup(on_scalar, ("u", UP, s + 2), TENSOR_COLS, HALF)
            second_products(UP, s, [0])
            quantise(("u", UP, s), HALF, PIECE)
            second_products(UP, s, [1])
            if s + 1 < U_PIECES:
                quantise(("u", UP, s + 1), 0, HALF)
            if s + 1 < U_PIECES:
                second_grouped_part(("u", UP, s + 1))
                regroup(on_scalar, ("u", UP, s + 1), HALF, GPSIMD_FROM)
                regroup_on_gpsimd(("u", UP, s + 1), GPSIMD_FROM, PIECE)
            multiply_and_store(s, PIECE if s + 2 < U_PIECES else BANK)
